import numpy as np
import ml_dtypes


def mxq(x, axis, fmt="e4m3"):
    dtype, down = {"e4m3": (ml_dtypes.float8_e4m3fn, 7), "e5m2": (ml_dtypes.float8_e5m2, 14)}[fmt]
    v = np.moveaxis(np.asarray(x, np.float32).astype(ml_dtypes.bfloat16).astype(np.float64), axis, -1)
    blocks = v.reshape(v.shape[:-1] + (-1, 32))
    amax = np.abs(blocks).max(-1, keepdims=True)
    byte = np.maximum(np.where(amax > 0, np.frexp(amax)[1] - 1 + 127, 0) - down, 1)
    scale = np.exp2(byte - 127.0)
    codes = (blocks / scale).astype(np.float32).astype(dtype).astype(np.float64)
    return np.moveaxis((codes * scale).reshape(v.shape), -1, axis)


WIDE = False


def mx_kscale(k):
    if not WIDE:
        return np.ones(k)
    levels = np.array([20, -20, 10, -10, 0])
    a = np.random.permutation(np.resize(levels, k // 512 * 4)).reshape(k // 512, 4)
    idx = np.arange(k)
    return np.exp2(a[idx // 512, idx % 128 // 32])


BF16 = ml_dtypes.bfloat16


def bf(x):
    return np.asarray(x, np.float32).astype(BF16)


def f64(x):
    return np.asarray(x).astype(np.float64)


B, U, I, H = 1024, 2, 512, 512


def sigmoid(v):
    return 1.0 / (1.0 + np.exp(-v))


def gru_parts(inputs, hidden, w_ih, w_hh, b_ih, b_hh):
    gx = (f64(inputs).transpose(1, 0, 2) @ f64(w_ih).transpose(0, 2, 1)).transpose(1, 0, 2) + f64(b_ih)
    gh = (f64(hidden).transpose(1, 0, 2) @ f64(w_hh).transpose(0, 2, 1)).transpose(1, 0, 2) + f64(b_hh)
    xr, xz, xn = gx[..., :H], gx[..., H:2 * H], gx[..., 2 * H:]
    hr, hz, hn = gh[..., :H], gh[..., H:2 * H], gh[..., 2 * H:]
    r = sigmoid(xr + hr)
    z = sigmoid(xz + hz)
    n = np.tanh(xn + r * hn)
    return r, z, n, hn


def setup_inputs():
    s = mx_kscale(B)[:, None, None]
    x0 = bf(np.random.standard_normal((B, U, I)))
    hidden = bf(np.random.standard_normal((B, U, H)))
    w_ih = bf(np.random.standard_normal((U, 3 * H, I)) / np.sqrt(I))
    w_hh = bf(np.random.standard_normal((U, 3 * H, H)) / np.sqrt(H))
    b_ih = bf(np.random.standard_normal((U, 3 * H)) * 0.3)
    b_hh = bf(np.random.standard_normal((U, 3 * H)) * 0.3)
    g = bf(np.random.standard_normal((B, U, H)) * np.exp2(np.random.randint(-12, 1, (B, U, 1))) * 4.0 / s)
    r, z, n, hn = gru_parts(x0, hidden, w_ih, w_hh, b_ih, b_hh)
    gates = np.concatenate([r, z, n], axis=-1)
    return {"inputs": bf(f64(x0) * s), "hidden": hidden, "w_ih": w_ih, "w_hh": w_hh, "b_ih": b_ih, "b_hh": b_hh,
            "gates": np.asarray(gates, np.float32), "hn": np.asarray(hn, np.float32), "grad_out": g}


def reference(inputs, hidden, w_ih, w_hh, b_ih, b_hh, gates, hn, grad_out):
    g = f64(grad_out)
    h = f64(hidden)
    ga = f64(gates)
    r, z, n = ga[..., :H], ga[..., H:2 * H], ga[..., 2 * H:]
    dn = g * (1.0 - z) * (1.0 - n * n)
    dz = g * (h - n) * z * (1.0 - z)
    dr = dn * f64(hn) * r * (1.0 - r)
    dgx = np.concatenate([dr, dz, dn], axis=-1)
    return mxq(dgx, 0, "e5m2").transpose(1, 2, 0) @ mxq(f64(inputs), 0, "e4m3").transpose(1, 0, 2)

@@ -1,0 +1,154 @@
+import concourse.mybir as mybir
+
+F32 = mybir.dt.float32
+BF16 = mybir.dt.bfloat16
+U32 = mybir.dt.uint32
+U8 = mybir.dt.uint8
+E4M3_X4 = mybir.dt.float8_e4m3fn_x4
+E5M2_X4 = mybir.dt.float8_e5m2_x4
+ALU = mybir.AluOpType
+ACT = mybir.ActivationFunctionType
+
+B, U, I, H = 1024, 2, 512, 512
+GATES = 3
+DR, DZ, DN = 0, 1, 2
+P = 128
+PACK = 4
+K_PASS = P * PACK
+PASSES = B // K_PASS
+RUN = 4
+
+FLOPS = 2 * U * GATES * H * I * B
+BYTES = 2 * 3 * B * U * H + 4 * B * U * (GATES + 1) * H + 4 * U * GATES * H * I
+
+
+def by_runs(rows):
+    return rows.rearrange("p j (c i) -> p c j i", i=RUN)
+
+
+def grouped_by_runs(grouped):
+    return grouped.rearrange("p (c i) j -> p c j i", i=RUN)
+
+
+def quantise(nc, codes, scales, grouped):
+    nc.vector.quantize_mx(out=codes, scales=scales, in_=grouped.rearrange("p w j -> p (w j)"))
+
+
+def tile_grouptorchgru_v_kernel(
+    tc, inputs, hidden, w_ih, w_hh, b_ih, b_hh, gates, hn, grad_out, out
+):
+    nc = tc.nc
+
+    def by_pass(dram):
+        return dram.rearrange("(c p j) u w -> c u p j w", c=PASSES, p=P, j=PACK)
+
+    x_dram = by_pass(inputs)
+    h_dram = by_pass(hidden)
+    g_dram = by_pass(grad_out)
+    hn_dram = by_pass(hn)
+    gates_dram = gates.rearrange("(c p j) u (s w) -> s c u p j w", c=PASSES, p=P, j=PACK, s=GATES)
+
+    def flat(rows):
+        return rows[:].rearrange("p j w -> p (j w)")
+
+    with (
+        tc.tile_pool(name="loads", bufs=2) as loads,
+        tc.tile_pool(name="work", bufs=1) as work,
+        tc.tile_pool(name="stage", bufs=4) as stage,
+        tc.tile_pool(name="keep", bufs=2) as keep,
+        tc.tile_pool(name="results", bufs=6) as results,
+        tc.psum_pool(name="psum", bufs=8) as psum,
+    ):
+        for u in range(U):
+            dgx_codes = keep.tile([P, PASSES, GATES * H], U32, align_bytes=64)
+            dgx_scales = keep.tile([P, PASSES, GATES * H], U8, align_bytes=64)
+            x_codes = keep.tile([P, PASSES, I], U32, align_bytes=64)
+            x_scales = keep.tile([P, PASSES, I], U8, align_bytes=64)
+
+            def finish_gate(gate, c, grouped):
+                gate_cols = slice(gate * H, (gate + 1) * H)
+                quantise(
+                    nc,
+                    dgx_codes[:, c, gate_cols].bitcast(E5M2_X4),
+                    dgx_scales[:, c, gate_cols],
+                    grouped[:],
+                )
+                if c < PASSES - 1:
+                    return
+                m_starts = range(gate * H, (gate + 1) * H, P)
+                accs = [psum.tile([P, I], F32, name="acc", tag="acc") for m0 in m_starts]
+                for k in range(PASSES):
+                    for m0, acc in zip(m_starts, accs):
+                        nc.tensor.matmul_mx(
+                            out=acc[:],
+                            lhsT=dgx_codes[:, k, m0 : m0 + P].bitcast(E5M2_X4),
+                            lhsT_scale=dgx_scales[:, k, m0 : m0 + P],
+                            rhs=x_codes[:, k, :].bitcast(E4M3_X4),
+                            rhs_scale=x_scales[:, k, :],
+                            start=(k == 0),
+                            stop=(k == PASSES - 1),
+                        )
+                sign = -1.0 if gate == DR else 1.0
+                for m0, acc in zip(m_starts, accs):
+                    result = results.tile([P, I], F32)
+                    nc.scalar.mul(out=result[:], in_=acc[:], mul=sign)
+                    nc.scalar.dma_start(out=out[u, m0 : m0 + P, :], in_=result[:])
+
+            for c in range(PASSES):
+                z = loads.tile([P, PACK, H], F32)
+                g = loads.tile([P, PACK, H], BF16)
+                n = loads.tile([P, PACK, H], F32)
+                h = loads.tile([P, PACK, H], BF16)
+                r = loads.tile([P, PACK, H], F32)
+                hn_rows = loads.tile([P, PACK, H], F32)
+                x = loads.tile([P, PACK, I], BF16)
+                nc.sync.dma_start(out=z[:], in_=gates_dram[1, c, u])
+                nc.sync.dma_start(out=g[:], in_=g_dram[c, u])
+                nc.sync.dma_start(out=n[:], in_=gates_dram[2, c, u])
+                nc.sync.dma_start(out=h[:], in_=h_dram[c, u])
+                nc.sync.dma_start(out=r[:], in_=gates_dram[0, c, u])
+                nc.sync.dma_start(out=hn_rows[:], in_=hn_dram[c, u])
+                nc.sync.dma_start(out=x[:], in_=x_dram[c, u])
+
+                nn = work.tile([P, PACK, H], F32)
+                nc.scalar.activation(out=flat(nn), in_=flat(n), func=ACT.Square)
+                sq = work.tile([P, PACK, H], F32)
+                nc.scalar.activation(out=flat(sq), in_=flat(r), func=ACT.Square, bias=-0.5)
+                x_grouped = stage.tile([P, I, PACK], BF16, tag="grouped", align_bytes=64)
+                nc.scalar.copy(out=grouped_by_runs(x_grouped[:]), in_=by_runs(x[:]))
+
+                m = work.tile([P, PACK, H], F32)
+                nc.vector.scalar_tensor_tensor(
+                    out=flat(m), in0=flat(z), scalar=1.0, in1=flat(g),
+                    op0=ALU.subtract, op1=ALU.mult,
+                )
+                d = work.tile([P, PACK, H], F32)
+                nc.vector.tensor_tensor(out=flat(d), in0=flat(n), in1=flat(h), op=ALU.subtract)
+                mz = work.tile([P, PACK, H], F32)
+                nc.vector.tensor_tensor(out=flat(mz), in0=flat(m), in1=flat(z), op=ALU.mult)
+                dn = work.tile([P, PACK, H], F32)
+                nc.vector.scalar_tensor_tensor(
+                    out=flat(dn), in0=flat(nn), scalar=1.0, in1=flat(m),
+                    op0=ALU.subtract, op1=ALU.mult,
+                )
+                dn_grouped = stage.tile([P, H, PACK], BF16, tag="grouped", align_bytes=64)
+                nc.scalar.copy(out=grouped_by_runs(dn_grouped[:]), in_=by_runs(dn[:]))
+                dz_grouped = stage.tile([P, H, PACK], BF16, tag="grouped", align_bytes=64)
+                nc.vector.tensor_tensor(
+                    out=grouped_by_runs(dz_grouped[:]), in0=by_runs(mz[:]), in1=by_runs(d[:]),
+                    op=ALU.mult,
+                )
+                quantise(nc, x_codes[:, c, :].bitcast(E4M3_X4), x_scales[:, c, :], x_grouped[:])
+                hrr = work.tile([P, PACK, H], F32)
+                nc.vector.scalar_tensor_tensor(
+                    out=flat(hrr), in0=flat(sq), scalar=0.25, in1=flat(hn_rows),
+                    op0=ALU.subtract, op1=ALU.mult,
+                )
+                finish_gate(DZ, c, dz_grouped)
+                finish_gate(DN, c, dn_grouped)
+                dr_grouped = stage.tile([P, H, PACK], BF16, tag="grouped", align_bytes=64)
+                nc.vector.tensor_tensor(
+                    out=grouped_by_runs(dr_grouped[:]), in0=by_runs(dn[:]), in1=by_runs(hrr[:]),
+                    op=ALU.mult,
+                )
+                finish_gate(DR, c, dr_grouped)

@@ -16,28 +16,30 @@ P = 128
 PACK = 4
 K_PASS = P * PACK
 PASSES = B // K_PASS
+HALF = H // 2
 RUN = 4
 
 FLOPS = 2 * U * GATES * H * I * B
 BYTES = 2 * 3 * B * U * H + 4 * B * U * (GATES + 1) * H + 4 * U * GATES * H * I
 
 
+def flat(rows):
+    return rows[:].rearrange("p j w -> p (j w)")
+
+
 def by_runs(rows):
-    return rows.rearrange("p j (c i) -> p c j i", i=RUN)
+    return rows[:].rearrange("p j (c i) -> p c j i", i=RUN)
 
 
 def grouped_by_runs(grouped):
-    return grouped.rearrange("p (c i) j -> p c j i", i=RUN)
-
-
-def quantise(nc, codes, scales, grouped):
-    nc.vector.quantize_mx(out=codes, scales=scales, in_=grouped.rearrange("p w j -> p (w j)"))
+    return grouped[:].rearrange("p (c i) j -> p c j i", i=RUN)
 
 
 def tile_grouptorchgru_v_kernel(
     tc, inputs, hidden, w_ih, w_hh, b_ih, b_hh, gates, hn, grad_out, out
 ):
     nc = tc.nc
+    passes = range(PASSES)
 
     def by_pass(dram):
         return dram.rearrange("(c p j) u w -> c u p j w", c=PASSES, p=P, j=PACK)
@@ -48,107 +50,135 @@ def tile_grouptorchgru_v_kernel(
     hn_dram = by_pass(hn)
     gates_dram = gates.rearrange("(c p j) u (s w) -> s c u p j w", c=PASSES, p=P, j=PACK, s=GATES)
 
-    def flat(rows):
-        return rows[:].rearrange("p j w -> p (j w)")
-
     with (
-        tc.tile_pool(name="loads", bufs=2) as loads,
-        tc.tile_pool(name="work", bufs=1) as work,
-        tc.tile_pool(name="stage", bufs=4) as stage,
-        tc.tile_pool(name="keep", bufs=2) as keep,
+        tc.tile_pool(name="sbuf", bufs=1) as sbuf,
         tc.tile_pool(name="results", bufs=6) as results,
         tc.psum_pool(name="psum", bufs=8) as psum,
     ):
-        for u in range(U):
-            dgx_codes = keep.tile([P, PASSES, GATES * H], U32, align_bytes=64)
-            dgx_scales = keep.tile([P, PASSES, GATES * H], U8, align_bytes=64)
-            x_codes = keep.tile([P, PASSES, I], U32, align_bytes=64)
-            x_scales = keep.tile([P, PASSES, I], U8, align_bytes=64)
 
-            def finish_gate(gate, c, grouped):
-                gate_cols = slice(gate * H, (gate + 1) * H)
-                quantise(
-                    nc,
-                    dgx_codes[:, c, gate_cols].bitcast(E5M2_X4),
-                    dgx_scales[:, c, gate_cols],
-                    grouped[:],
+        def rows_per_pass(name, dtype):
+            return [sbuf.tile([P, PACK, H], dtype, name="%s%d" % (name, c)) for c in passes]
+
+        def grouped_per_pass(name):
+            return [
+                sbuf.tile([P, H, PACK], BF16, name="%s%d" % (name, c), align_bytes=64)
+                for c in passes
+            ]
+
+        for u in range(U):
+            z, n, r, hn_rows = [rows_per_pass(name, F32) for name in ("z", "n", "r", "hn")]
+            g, h, x = [rows_per_pass(name, BF16) for name in ("g", "h", "x")]
+            for c in passes:
+                nc.sync.dma_start(out=z[c][:], in_=gates_dram[1, c, u])
+                nc.sync.dma_start(out=g[c][:], in_=g_dram[c, u])
+            for c in passes:
+                nc.sync.dma_start(out=n[c][:], in_=gates_dram[2, c, u])
+                nc.sync.dma_start(out=h[c][:], in_=h_dram[c, u])
+            for c in passes:
+                nc.sync.dma_start(out=x[c][:], in_=x_dram[c, u])
+            for c in passes:
+                nc.sync.dma_start(out=r[c][:], in_=gates_dram[0, c, u])
+                nc.sync.dma_start(out=hn_rows[c][:], in_=hn_dram[c, u])
+
+            dgx_codes = sbuf.tile([P, PASSES, GATES * H], U32, align_bytes=64)
+            dgx_scales = sbuf.tile([P, PASSES, GATES * H], U8, align_bytes=64)
+            x_codes = sbuf.tile([P, PASSES, I], U32, align_bytes=64)
+            x_scales = sbuf.tile([P, PASSES, I], U8, align_bytes=64)
+
+            def quantise_gate(gate, c, grouped, first=0, width=H):
+                cols = slice(gate * H + first, gate * H + first + width)
+                nc.vector.quantize_mx(
+                    out=dgx_codes[:, c, cols].bitcast(E5M2_X4),
+                    scales=dgx_scales[:, c, cols],
+                    in_=grouped[:, first : first + width, :].rearrange("p w j -> p (w j)"),
                 )
-                if c < PASSES - 1:
-                    return
-                m_starts = range(gate * H, (gate + 1) * H, P)
+
+            def multiply_gate(gate, sign, first=0, width=H):
+                m_starts = range(gate * H + first, gate * H + first + width, P)
                 accs = [psum.tile([P, I], F32, name="acc", tag="acc") for m0 in m_starts]
-                for k in range(PASSES):
+                for c in passes:
                     for m0, acc in zip(m_starts, accs):
                         nc.tensor.matmul_mx(
                             out=acc[:],
-                            lhsT=dgx_codes[:, k, m0 : m0 + P].bitcast(E5M2_X4),
-                            lhsT_scale=dgx_scales[:, k, m0 : m0 + P],
-                            rhs=x_codes[:, k, :].bitcast(E4M3_X4),
-                            rhs_scale=x_scales[:, k, :],
-                            start=(k == 0),
-                            stop=(k == PASSES - 1),
+                            lhsT=dgx_codes[:, c, m0 : m0 + P].bitcast(E5M2_X4),
+                            lhsT_scale=dgx_scales[:, c, m0 : m0 + P],
+                            rhs=x_codes[:, c, :].bitcast(E4M3_X4),
+                            rhs_scale=x_scales[:, c, :],
+                            start=(c == 0),
+                            stop=(c == PASSES - 1),
                         )
-                sign = -1.0 if gate == DR else 1.0
                 for m0, acc in zip(m_starts, accs):
                     result = results.tile([P, I], F32)
                     nc.scalar.mul(out=result[:], in_=acc[:], mul=sign)
-                    nc.scalar.dma_start(out=out[u, m0 : m0 + P, :], in_=result[:])
+                    nc.sync.dma_start(out=out[u, m0 : m0 + P, :], in_=result[:])
 
-            for c in range(PASSES):
-                z = loads.tile([P, PACK, H], F32)
-                g = loads.tile([P, PACK, H], BF16)
-                n = loads.tile([P, PACK, H], F32)
-                h = loads.tile([P, PACK, H], BF16)
-                r = loads.tile([P, PACK, H], F32)
-                hn_rows = loads.tile([P, PACK, H], F32)
-                x = loads.tile([P, PACK, I], BF16)
-                nc.sync.dma_start(out=z[:], in_=gates_dram[1, c, u])
-                nc.sync.dma_start(out=g[:], in_=g_dram[c, u])
-                nc.sync.dma_start(out=n[:], in_=gates_dram[2, c, u])
-                nc.sync.dma_start(out=h[:], in_=h_dram[c, u])
-                nc.sync.dma_start(out=r[:], in_=gates_dram[0, c, u])
-                nc.sync.dma_start(out=hn_rows[:], in_=hn_dram[c, u])
-                nc.sync.dma_start(out=x[:], in_=x_dram[c, u])
+            dn = rows_per_pass("dn", F32)
+            x_grouped = grouped_per_pass("x_grouped")
+            hrr = rows_per_pass("hrr", F32)
+            for c in passes:
+                nc.scalar.activation(out=flat(dn[c]), in_=flat(n[c]), func=ACT.Square)
+            for c in passes:
+                nc.scalar.copy(out=grouped_by_runs(x_grouped[c]), in_=by_runs(x[c]))
+            for c in passes:
+                nc.scalar.activation(out=flat(hrr[c]), in_=flat(r[c]), func=ACT.Square, bias=-0.5)
 
-                nn = work.tile([P, PACK, H], F32)
-                nc.scalar.activation(out=flat(nn), in_=flat(n), func=ACT.Square)
-                sq = work.tile([P, PACK, H], F32)
-                nc.scalar.activation(out=flat(sq), in_=flat(r), func=ACT.Square, bias=-0.5)
-                x_grouped = stage.tile([P, I, PACK], BF16, tag="grouped", align_bytes=64)
-                nc.scalar.copy(out=grouped_by_runs(x_grouped[:]), in_=by_runs(x[:]))
-
-                m = work.tile([P, PACK, H], F32)
+            m = rows_per_pass("m", F32)
+            for c in passes:
                 nc.vector.scalar_tensor_tensor(
-                    out=flat(m), in0=flat(z), scalar=1.0, in1=flat(g),
+                    out=flat(m[c]), in0=flat(z[c]), scalar=1.0, in1=flat(g[c]),
                     op0=ALU.subtract, op1=ALU.mult,
                 )
-                d = work.tile([P, PACK, H], F32)
-                nc.vector.tensor_tensor(out=flat(d), in0=flat(n), in1=flat(h), op=ALU.subtract)
-                mz = work.tile([P, PACK, H], F32)
-                nc.vector.tensor_tensor(out=flat(mz), in0=flat(m), in1=flat(z), op=ALU.mult)
-                dn = work.tile([P, PACK, H], F32)
-                nc.vector.scalar_tensor_tensor(
-                    out=flat(dn), in0=flat(nn), scalar=1.0, in1=flat(m),
-                    op0=ALU.subtract, op1=ALU.mult,
-                )
-                dn_grouped = stage.tile([P, H, PACK], BF16, tag="grouped", align_bytes=64)
-                nc.scalar.copy(out=grouped_by_runs(dn_grouped[:]), in_=by_runs(dn[:]))
-                dz_grouped = stage.tile([P, H, PACK], BF16, tag="grouped", align_bytes=64)
+            mz = z
+            for c in passes:
+                nc.vector.tensor_tensor(out=flat(mz[c]), in0=flat(m[c]), in1=flat(z[c]), op=ALU.mult)
+            d = n
+            for c in passes:
+                nc.vector.tensor_tensor(out=flat(d[c]), in0=flat(n[c]), in1=flat(h[c]), op=ALU.subtract)
+            dz_grouped = grouped_per_pass("dz_grouped")
+            for c in passes:
                 nc.vector.tensor_tensor(
-                    out=grouped_by_runs(dz_grouped[:]), in0=by_runs(mz[:]), in1=by_runs(d[:]),
+                    out=grouped_by_runs(dz_grouped[c]), in0=by_runs(mz[c]), in1=by_runs(d[c]),
                     op=ALU.mult,
                 )
-                quantise(nc, x_codes[:, c, :].bitcast(E4M3_X4), x_scales[:, c, :], x_grouped[:])
-                hrr = work.tile([P, PACK, H], F32)
+            for c in passes:
+                nc.vector.quantize_mx(
+                    out=x_codes[:, c, :].bitcast(E4M3_X4),
+                    scales=x_scales[:, c, :],
+                    in_=x_grouped[c][:].rearrange("p w j -> p (w j)"),
+                )
+            for c in passes:
+                quantise_gate(DZ, c, dz_grouped[c])
+            multiply_gate(DZ, 1.0)
+
+            dn_grouped = grouped_per_pass("dn_grouped")
+            for c in passes:
                 nc.vector.scalar_tensor_tensor(
-                    out=flat(hrr), in0=flat(sq), scalar=0.25, in1=flat(hn_rows),
+                    out=flat(dn[c]), in0=flat(dn[c]), scalar=1.0, in1=flat(m[c]),
                     op0=ALU.subtract, op1=ALU.mult,
                 )
-                finish_gate(DZ, c, dz_grouped)
-                finish_gate(DN, c, dn_grouped)
-                dr_grouped = stage.tile([P, H, PACK], BF16, tag="grouped", align_bytes=64)
+                nc.scalar.copy(out=grouped_by_runs(dn_grouped[c]), in_=by_runs(dn[c]))
+            for c in passes:
+                nc.vector.scalar_tensor_tensor(
+                    out=flat(hrr[c]), in0=flat(hrr[c]), scalar=0.25, in1=flat(hn_rows[c]),
+                    op0=ALU.subtract, op1=ALU.mult,
+                )
+            for c in passes:
+                quantise_gate(DN, c, dn_grouped[c])
+            multiply_gate(DN, 1.0)
+
+            dr_grouped = grouped_per_pass("dr_grouped")
+            halves = [(c, first) for c in passes for first in range(0, H, HALF)]
+            for i, (c, first) in enumerate(halves):
+                cols = slice(first, first + HALF)
                 nc.vector.tensor_tensor(
-                    out=grouped_by_runs(dr_grouped[:]), in0=by_runs(dn[:]), in1=by_runs(hrr[:]),
+                    out=grouped_by_runs(dr_grouped[c][:, cols, :]),
+                    in0=by_runs(dn[c][:, :, cols]),
+                    in1=by_runs(hrr[c][:, :, cols]),
                     op=ALU.mult,
                 )
-                finish_gate(DR, c, dr_grouped)
+                if i > 0:
+                    c_before, first_before = halves[i - 1]
+                    quantise_gate(DR, c_before, dr_grouped[c_before], first_before, HALF)
+            quantise_gate(DR, c, dr_grouped[c], first, HALF)
+            for first in range(0, H, HALF):
+                multiply_gate(DR, -1.0, first, HALF)

@@ -16,7 +16,6 @@ P = 128
 PACK = 4
 K_PASS = P * PACK
 PASSES = B // K_PASS
-HALF = H // 2
 RUN = 4
 
 FLOPS = 2 * U * GATES * H * I * B
@@ -35,11 +34,20 @@ def grouped_by_runs(grouped):
     return grouped[:].rearrange("p (c i) j -> p c j i", i=RUN)
 
 
+def one_behind(pieces, produce, consume):
+    for i, piece in enumerate(pieces):
+        produce(*piece)
+        if i > 0:
+            consume(*pieces[i - 1])
+    consume(*pieces[-1])
+
+
 def tile_grouptorchgru_v_kernel(
     tc, inputs, hidden, w_ih, w_hh, b_ih, b_hh, gates, hn, grad_out, out
 ):
     nc = tc.nc
     passes = range(PASSES)
+    half_passes = [(c, slice(j, j + PACK // 2)) for c in passes for j in range(0, PACK, PACK // 2)]
 
     def by_pass(dram):
         return dram.rearrange("(c p j) u w -> c u p j w", c=PASSES, p=P, j=PACK)
@@ -68,9 +76,9 @@ def tile_grouptorchgru_v_kernel(
         for u in range(U):
             z, n, r, hn_rows = [rows_per_pass(name, F32) for name in ("z", "n", "r", "hn")]
             g, h, x = [rows_per_pass(name, BF16) for name in ("g", "h", "x")]
-            for c in passes:
-                nc.sync.dma_start(out=z[c][:], in_=gates_dram[1, c, u])
-                nc.sync.dma_start(out=g[c][:], in_=g_dram[c, u])
+            for c, rows in half_passes:
+                nc.sync.dma_start(out=z[c][:, rows, :], in_=gates_dram[1, c, u][:, rows, :])
+                nc.sync.dma_start(out=g[c][:, rows, :], in_=g_dram[c, u][:, rows, :])
             for c in passes:
                 nc.sync.dma_start(out=n[c][:], in_=gates_dram[2, c, u])
                 nc.sync.dma_start(out=h[c][:], in_=h_dram[c, u])
@@ -123,14 +131,21 @@ def tile_grouptorchgru_v_kernel(
                 nc.scalar.activation(out=flat(hrr[c]), in_=flat(r[c]), func=ACT.Square, bias=-0.5)
 
             m = rows_per_pass("m", F32)
-            for c in passes:
-                nc.vector.scalar_tensor_tensor(
-                    out=flat(m[c]), in0=flat(z[c]), scalar=1.0, in1=flat(g[c]),
-                    op0=ALU.subtract, op1=ALU.mult,
-                )
             mz = z
-            for c in passes:
-                nc.vector.tensor_tensor(out=flat(mz[c]), in0=flat(m[c]), in1=flat(z[c]), op=ALU.mult)
+
+            def make_m(c, rows):
+                nc.vector.scalar_tensor_tensor(
+                    out=flat(m[c][:, rows, :]), in0=flat(z[c][:, rows, :]), scalar=1.0,
+                    in1=flat(g[c][:, rows, :]), op0=ALU.subtract, op1=ALU.mult,
+                )
+
+            def make_mz(c, rows):
+                nc.vector.tensor_tensor(
+                    out=flat(mz[c][:, rows, :]), in0=flat(m[c][:, rows, :]),
+                    in1=flat(z[c][:, rows, :]), op=ALU.mult,
+                )
+
+            one_behind(half_passes, make_m, make_mz)
             d = n
             for c in passes:
                 nc.vector.tensor_tensor(out=flat(d[c]), in0=flat(n[c]), in1=flat(h[c]), op=ALU.subtract)
@@ -167,18 +182,21 @@ def tile_grouptorchgru_v_kernel(
             multiply_gate(DN, 1.0)
 
             dr_grouped = grouped_per_pass("dr_grouped")
-            halves = [(c, first) for c in passes for first in range(0, H, HALF)]
-            for i, (c, first) in enumerate(halves):
-                cols = slice(first, first + HALF)
+
+            def make_dr(c, first, width):
+                cols = slice(first, first + width)
                 nc.vector.tensor_tensor(
                     out=grouped_by_runs(dr_grouped[c][:, cols, :]),
                     in0=by_runs(dn[c][:, :, cols]),
                     in1=by_runs(hrr[c][:, :, cols]),
                     op=ALU.mult,
                 )
-                if i > 0:
-                    c_before, first_before = halves[i - 1]
-                    quantise_gate(DR, c_before, dr_grouped[c_before], first_before, HALF)
-            quantise_gate(DR, c, dr_grouped[c], first, HALF)
-            for first in range(0, H, HALF):
-                multiply_gate(DR, -1.0, first, HALF)
+
+            def quantise_dr(c, first, width):
+                quantise_gate(DR, c, dr_grouped[c], first, width)
+
+            whole_passes = [(c, 0, H) for c in passes[:-1]]
+            tiles_of_last_pass = [(passes[-1], first, P) for first in range(0, H, P)]
+            one_behind(whole_passes + tiles_of_last_pass, make_dr, quantise_dr)
+            for first in range(0, H, P):
+                multiply_gate(DR, -1.0, first, P)

@@ -1,4 +1,5 @@
 import concourse.mybir as mybir
+from concourse.masks import make_identity
 
 F32 = mybir.dt.float32
 BF16 = mybir.dt.bfloat16
@@ -16,6 +17,7 @@ P = 128
 PACK = 4
 K_PASS = P * PACK
 PASSES = B // K_PASS
+TILES_OF_A_UNIT = GATES * H // P
 RUN = 4
 
 FLOPS = 2 * U * GATES * H * I * B
@@ -47,7 +49,10 @@ def tile_grouptorchgru_v_kernel(
 ):
     nc = tc.nc
     passes = range(PASSES)
-    half_passes = [(c, slice(j, j + PACK // 2)) for c in passes for j in range(0, PACK, PACK // 2)]
+    last_pass = PASSES - 1
+    row_halves = [slice(j, j + PACK // 2) for j in range(0, PACK, PACK // 2)]
+    half_passes = [(c, rows) for c in passes for rows in row_halves]
+    column_tiles = [slice(first, first + P) for first in range(0, H, P)]
 
     def by_pass(dram):
         return dram.rearrange("(c p j) u w -> c u p j w", c=PASSES, p=P, j=PACK)
@@ -60,8 +65,9 @@ def tile_grouptorchgru_v_kernel(
 
     with (
         tc.tile_pool(name="sbuf", bufs=1) as sbuf,
-        tc.tile_pool(name="results", bufs=6) as results,
-        tc.psum_pool(name="psum", bufs=8) as psum,
+        tc.tile_pool(name="results", bufs=TILES_OF_A_UNIT) as results,
+        tc.psum_pool(name="psum", bufs=4) as psum,
+        tc.manual_schedule(),
     ):
 
         def rows_per_pass(name, dtype):
@@ -73,62 +79,97 @@ def tile_grouptorchgru_v_kernel(
                 for c in passes
             ]
 
-        for u in range(U):
-            z, n, r, hn_rows = [rows_per_pass(name, F32) for name in ("z", "n", "r", "hn")]
-            g, h, x = [rows_per_pass(name, BF16) for name in ("g", "h", "x")]
-            for c, rows in half_passes:
-                nc.sync.dma_start(out=z[c][:, rows, :], in_=gates_dram[1, c, u][:, rows, :])
-                nc.sync.dma_start(out=g[c][:, rows, :], in_=g_dram[c, u][:, rows, :])
+        def load_z_g_x_n_h(u):
+            z, n = [rows_per_pass(name, F32) for name in ("z", "n")]
+            g, x, h = [rows_per_pass(name, BF16) for name in ("g", "x", "h")]
+            for c in passes:
+                for rows in row_halves:
+                    nc.sync.dma_start(out=z[c][:, rows, :], in_=gates_dram[1, c, u][:, rows, :])
+                    nc.sync.dma_start(out=g[c][:, rows, :], in_=g_dram[c, u][:, rows, :])
+                nc.sync.dma_start(out=x[c][:], in_=x_dram[c, u])
             for c in passes:
                 nc.sync.dma_start(out=n[c][:], in_=gates_dram[2, c, u])
                 nc.sync.dma_start(out=h[c][:], in_=h_dram[c, u])
-            for c in passes:
-                nc.sync.dma_start(out=x[c][:], in_=x_dram[c, u])
+            return z, g, x, n, h
+
+        def load_r_hn(u):
+            r, hn_rows = [rows_per_pass(name, F32) for name in ("r", "hn")]
             for c in passes:
                 nc.sync.dma_start(out=r[c][:], in_=gates_dram[0, c, u])
                 nc.sync.dma_start(out=hn_rows[c][:], in_=hn_dram[c, u])
+            return r, hn_rows
 
+        def regroup_x_and_square_n(x, n):
+            x_grouped = grouped_per_pass("x_grouped")
+            dn = rows_per_pass("dn", F32)
+            for c in passes:
+                nc.scalar.copy(out=grouped_by_runs(x_grouped[c]), in_=by_runs(x[c]))
+            for c in passes:
+                nc.scalar.activation(out=flat(dn[c]), in_=flat(n[c]), func=ACT.Square)
+            return x_grouped, dn
+
+        identity = sbuf.tile([P, P], F32)
+        make_identity(nc, identity[:])
+        minus_identity = sbuf.tile([P, P], BF16)
+        nc.scalar.mul(out=minus_identity[:], in_=identity[:], mul=-1.0)
+
+        z, g, x, n, h = load_z_g_x_n_h(0)
+        r, hn_rows = load_r_hn(0)
+        x_grouped, dn = regroup_x_and_square_n(x, n)
+
+        for u in range(U):
+            another_unit = u + 1 < U
             dgx_codes = sbuf.tile([P, PASSES, GATES * H], U32, align_bytes=64)
             dgx_scales = sbuf.tile([P, PASSES, GATES * H], U8, align_bytes=64)
             x_codes = sbuf.tile([P, PASSES, I], U32, align_bytes=64)
             x_scales = sbuf.tile([P, PASSES, I], U8, align_bytes=64)
 
-            def quantise_gate(gate, c, grouped, first=0, width=H):
-                cols = slice(gate * H + first, gate * H + first + width)
+            def quantise(gate, c, grouped, cols=slice(0, H)):
+                first = gate * H
                 nc.vector.quantize_mx(
-                    out=dgx_codes[:, c, cols].bitcast(E5M2_X4),
-                    scales=dgx_scales[:, c, cols],
-                    in_=grouped[:, first : first + width, :].rearrange("p w j -> p (w j)"),
+                    out=dgx_codes[:, c, first:][:, cols].bitcast(E5M2_X4),
+                    scales=dgx_scales[:, c, first:][:, cols],
+                    in_=grouped[:, cols, :].rearrange("p w j -> p (w j)"),
                 )
 
-            def multiply_gate(gate, sign, first=0, width=H):
-                m_starts = range(gate * H + first, gate * H + first + width, P)
-                accs = [psum.tile([P, I], F32, name="acc", tag="acc") for m0 in m_starts]
-                for c in passes:
-                    for m0, acc in zip(m_starts, accs):
-                        nc.tensor.matmul_mx(
-                            out=acc[:],
-                            lhsT=dgx_codes[:, c, m0 : m0 + P].bitcast(E5M2_X4),
-                            lhsT_scale=dgx_scales[:, c, m0 : m0 + P],
-                            rhs=x_codes[:, c, :].bitcast(E4M3_X4),
-                            rhs_scale=x_scales[:, c, :],
-                            start=(c == 0),
-                            stop=(c == PASSES - 1),
-                        )
-                for m0, acc in zip(m_starts, accs):
-                    result = results.tile([P, I], F32)
-                    nc.scalar.mul(out=result[:], in_=acc[:], mul=sign)
-                    nc.sync.dma_start(out=out[u, m0 : m0 + P, :], in_=result[:])
+            def open_banks():
+                return [psum.tile([P, I], F32, name="acc", tag="acc") for cols in column_tiles]
 
-            dn = rows_per_pass("dn", F32)
-            x_grouped = grouped_per_pass("x_grouped")
-            hrr = rows_per_pass("hrr", F32)
-            for c in passes:
-                nc.scalar.activation(out=flat(dn[c]), in_=flat(n[c]), func=ACT.Square)
-            for c in passes:
-                nc.scalar.copy(out=grouped_by_runs(x_grouped[c]), in_=by_runs(x[c]))
-            for c in passes:
-                nc.scalar.activation(out=flat(hrr[c]), in_=flat(r[c]), func=ACT.Square, bias=-0.5)
+            def multiply(gate, c, acc, cols):
+                first = gate * H
+                nc.tensor.matmul_mx(
+                    out=acc[:],
+                    lhsT=dgx_codes[:, c, first:][:, cols].bitcast(E5M2_X4),
+                    lhsT_scale=dgx_scales[:, c, first:][:, cols],
+                    rhs=x_codes[:, c, :].bitcast(E4M3_X4),
+                    rhs_scale=x_scales[:, c, :],
+                    start=(c == 0),
+                    stop=(c == last_pass),
+                )
+
+            def store(gate, sign, acc, cols):
+                result = results.tile([P, I], F32)
+                nc.scalar.mul(out=result[:], in_=acc[:], mul=sign)
+                nc.sync.dma_start(out=out[u, gate * H :, :][cols, :], in_=result[:])
+
+            def quantise_multiply_store(gate, grouped):
+                accs = open_banks()
+                for c in passes:
+                    quantise(gate, c, grouped[c])
+                for c in passes:
+                    for acc, cols in zip(accs, column_tiles):
+                        multiply(gate, c, acc, cols)
+                for acc, cols in zip(accs, column_tiles):
+                    store(gate, 1.0, acc, cols)
+
+            d_banks = [psum.tile([P, PACK, P], F32, name="d_bank", tag="d_bank") for cols in column_tiles]
+            for d_bank, cols in zip(d_banks, column_tiles):
+                nc.tensor.matmul(
+                    out=d_bank[:], lhsT=identity[:], rhs=n[last_pass][:, :, cols], start=True, stop=False
+                )
+                nc.tensor.matmul(
+                    out=d_bank[:], lhsT=minus_identity[:], rhs=h[last_pass][:, :, cols], start=False, stop=True
+                )
 
             m = rows_per_pass("m", F32)
             mz = z
@@ -146,24 +187,16 @@ def tile_grouptorchgru_v_kernel(
                 )
 
             one_behind(half_passes, make_m, make_mz)
-            d = n
-            for c in passes:
-                nc.vector.tensor_tensor(out=flat(d[c]), in0=flat(n[c]), in1=flat(h[c]), op=ALU.subtract)
-            dz_grouped = grouped_per_pass("dz_grouped")
-            for c in passes:
-                nc.vector.tensor_tensor(
-                    out=grouped_by_runs(dz_grouped[c]), in0=by_runs(mz[c]), in1=by_runs(d[c]),
-                    op=ALU.mult,
-                )
             for c in passes:
                 nc.vector.quantize_mx(
                     out=x_codes[:, c, :].bitcast(E4M3_X4),
                     scales=x_scales[:, c, :],
                     in_=x_grouped[c][:].rearrange("p w j -> p (w j)"),
                 )
-            for c in passes:
-                quantise_gate(DZ, c, dz_grouped[c])
-            multiply_gate(DZ, 1.0)
+
+            d_rows = [sbuf.tile([P, PACK, H], F32, name="d%d" % c) for c in passes[:-1]]
+            for c in passes[:-1]:
+                nc.vector.tensor_tensor(out=flat(d_rows[c]), in0=flat(n[c]), in1=flat(h[c]), op=ALU.subtract)
 
             dn_grouped = grouped_per_pass("dn_grouped")
             for c in passes:
@@ -172,19 +205,42 @@ def tile_grouptorchgru_v_kernel(
                     op0=ALU.subtract, op1=ALU.mult,
                 )
                 nc.scalar.copy(out=grouped_by_runs(dn_grouped[c]), in_=by_runs(dn[c]))
+            hrr = rows_per_pass("hrr", F32)
+            for c in passes:
+                nc.scalar.activation(out=flat(hrr[c]), in_=flat(r[c]), func=ACT.Square, bias=-0.5)
+
+            dz_grouped = grouped_per_pass("dz_grouped")
+            for c in passes[:-1]:
+                nc.vector.tensor_tensor(
+                    out=grouped_by_runs(dz_grouped[c]), in0=by_runs(mz[c]), in1=by_runs(d_rows[c]),
+                    op=ALU.mult,
+                )
+            for d_bank, cols in zip(d_banks, column_tiles):
+                nc.vector.tensor_tensor(
+                    out=grouped_by_runs(dz_grouped[last_pass][:, cols, :]),
+                    in0=by_runs(mz[last_pass][:, :, cols]),
+                    in1=by_runs(d_bank),
+                    op=ALU.mult,
+                )
+            if another_unit:
+                next_z_g_x_n_h = load_z_g_x_n_h(u + 1)
+
+            quantise_multiply_store(DN, dn_grouped)
+            quantise_multiply_store(DZ, dz_grouped)
+
             for c in passes:
                 nc.vector.scalar_tensor_tensor(
                     out=flat(hrr[c]), in0=flat(hrr[c]), scalar=0.25, in1=flat(hn_rows[c]),
                     op0=ALU.subtract, op1=ALU.mult,
                 )
-            for c in passes:
-                quantise_gate(DN, c, dn_grouped[c])
-            multiply_gate(DN, 1.0)
+            if another_unit:
+                next_r_hn = load_r_hn(u + 1)
 
             dr_grouped = grouped_per_pass("dr_grouped")
+            dr_accs = open_banks()
 
-            def make_dr(c, first, width):
-                cols = slice(first, first + width)
+            def make_dr(c, tiles):
+                cols = slice(tiles[0] * P, (tiles[-1] + 1) * P)
                 nc.vector.tensor_tensor(
                     out=grouped_by_runs(dr_grouped[c][:, cols, :]),
                     in0=by_runs(dn[c][:, :, cols]),
@@ -192,11 +248,19 @@ def tile_grouptorchgru_v_kernel(
                     op=ALU.mult,
                 )
 
-            def quantise_dr(c, first, width):
-                quantise_gate(DR, c, dr_grouped[c], first, width)
+            def finish_dr(c, tiles):
+                quantise(DR, c, dr_grouped[c], slice(tiles[0] * P, (tiles[-1] + 1) * P))
+                for t in tiles:
+                    multiply(DR, c, dr_accs[t], column_tiles[t])
+                    if c == last_pass:
+                        store(DR, -1.0, dr_accs[t], column_tiles[t])
 
-            whole_passes = [(c, 0, H) for c in passes[:-1]]
-            tiles_of_last_pass = [(passes[-1], first, P) for first in range(0, H, P)]
-            one_behind(whole_passes + tiles_of_last_pass, make_dr, quantise_dr)
-            for first in range(0, H, P):
-                multiply_gate(DR, -1.0, first, P)
+            all_tiles = list(range(len(column_tiles)))
+            whole_passes = [(c, all_tiles) for c in passes[:-1]]
+            tiles_of_last_pass = [(last_pass, [t]) for t in all_tiles]
+            one_behind(whole_passes + tiles_of_last_pass, make_dr, finish_dr)
+
+            if another_unit:
+                z, g, x, n, h = next_z_g_x_n_h
+                r, hn_rows = next_r_hn
+                x_grouped, dn = regroup_x_and_square_n(x, n)

@@ -49,15 +49,17 @@ def tile_grouptorchgru_v_kernel(
 ):
     nc = tc.nc
     passes = range(PASSES)
+    units = range(U)
     last_pass = PASSES - 1
     row_halves = [slice(j, j + PACK // 2) for j in range(0, PACK, PACK // 2)]
     half_passes = [(c, rows) for c in passes for rows in row_halves]
     column_tiles = [slice(first, first + P) for first in range(0, H, P)]
+    all_tiles = list(range(len(column_tiles)))
 
     def by_pass(dram):
         return dram.rearrange("(c p j) u w -> c u p j w", c=PASSES, p=P, j=PACK)
 
-    x_dram = by_pass(inputs)
+    x_dram = inputs.rearrange("(c p j) u w -> c p j u w", c=PASSES, p=P, j=PACK)
     h_dram = by_pass(hidden)
     g_dram = by_pass(grad_out)
     hn_dram = by_pass(hn)
@@ -79,18 +81,17 @@ def tile_grouptorchgru_v_kernel(
                 for c in passes
             ]
 
-        def load_z_g_x_n_h(u):
+        def load_z_g_n_h(u):
             z, n = [rows_per_pass(name, F32) for name in ("z", "n")]
-            g, x, h = [rows_per_pass(name, BF16) for name in ("g", "x", "h")]
+            g, h = [rows_per_pass(name, BF16) for name in ("g", "h")]
             for c in passes:
                 for rows in row_halves:
                     nc.sync.dma_start(out=z[c][:, rows, :], in_=gates_dram[1, c, u][:, rows, :])
                     nc.sync.dma_start(out=g[c][:, rows, :], in_=g_dram[c, u][:, rows, :])
-                nc.sync.dma_start(out=x[c][:], in_=x_dram[c, u])
             for c in passes:
                 nc.sync.dma_start(out=n[c][:], in_=gates_dram[2, c, u])
                 nc.sync.dma_start(out=h[c][:], in_=h_dram[c, u])
-            return z, g, x, n, h
+            return z, g, n, h
 
         def load_r_hn(u):
             r, hn_rows = [rows_per_pass(name, F32) for name in ("r", "hn")]
@@ -99,30 +100,40 @@ def tile_grouptorchgru_v_kernel(
                 nc.sync.dma_start(out=hn_rows[c][:], in_=hn_dram[c, u])
             return r, hn_rows
 
-        def regroup_x_and_square_n(x, n):
-            x_grouped = grouped_per_pass("x_grouped")
+        def square_n(n):
             dn = rows_per_pass("dn", F32)
             for c in passes:
-                nc.scalar.copy(out=grouped_by_runs(x_grouped[c]), in_=by_runs(x[c]))
-            for c in passes:
                 nc.scalar.activation(out=flat(dn[c]), in_=flat(n[c]), func=ACT.Square)
-            return x_grouped, dn
+            return dn
 
         identity = sbuf.tile([P, P], F32)
         make_identity(nc, identity[:])
         minus_identity = sbuf.tile([P, P], BF16)
         nc.scalar.mul(out=minus_identity[:], in_=identity[:], mul=-1.0)
 
-        z, g, x, n, h = load_z_g_x_n_h(0)
+        z, g, n, h = load_z_g_n_h(0)
         r, hn_rows = load_r_hn(0)
-        x_grouped, dn = regroup_x_and_square_n(x, n)
+        x = [sbuf.tile([P, PACK, U, I], BF16, name="x%d" % c) for c in passes]
+        for c in passes:
+            nc.sync.dma_start(out=x[c][:], in_=x_dram[c])
+        dn = square_n(n)
 
-        for u in range(U):
+        x_grouped = [grouped_per_pass("x_grouped_%d_" % u) for u in units]
+        x_codes = sbuf.tile([P, U, PASSES, I], U32, align_bytes=64)
+        x_scales = sbuf.tile([P, U, PASSES, I], U8, align_bytes=64)
+
+        def quantise_x(u):
+            for c in passes:
+                nc.vector.quantize_mx(
+                    out=x_codes[:, u, c, :].bitcast(E4M3_X4),
+                    scales=x_scales[:, u, c, :],
+                    in_=x_grouped[u][c][:].rearrange("p w j -> p (w j)"),
+                )
+
+        for u in units:
             another_unit = u + 1 < U
             dgx_codes = sbuf.tile([P, PASSES, GATES * H], U32, align_bytes=64)
             dgx_scales = sbuf.tile([P, PASSES, GATES * H], U8, align_bytes=64)
-            x_codes = sbuf.tile([P, PASSES, I], U32, align_bytes=64)
-            x_scales = sbuf.tile([P, PASSES, I], U8, align_bytes=64)
 
             def quantise(gate, c, grouped, cols=slice(0, H)):
                 first = gate * H
@@ -141,8 +152,8 @@ def tile_grouptorchgru_v_kernel(
                     out=acc[:],
                     lhsT=dgx_codes[:, c, first:][:, cols].bitcast(E5M2_X4),
                     lhsT_scale=dgx_scales[:, c, first:][:, cols],
-                    rhs=x_codes[:, c, :].bitcast(E4M3_X4),
-                    rhs_scale=x_scales[:, c, :],
+                    rhs=x_codes[:, u, c, :].bitcast(E4M3_X4),
+                    rhs_scale=x_scales[:, u, c, :],
                     start=(c == 0),
                     stop=(c == last_pass),
                 )
@@ -152,15 +163,13 @@ def tile_grouptorchgru_v_kernel(
                 nc.scalar.mul(out=result[:], in_=acc[:], mul=sign)
                 nc.sync.dma_start(out=out[u, gate * H :, :][cols, :], in_=result[:])
 
-            def quantise_multiply_store(gate, grouped):
+            def multiply_store(gate, sign):
                 accs = open_banks()
-                for c in passes:
-                    quantise(gate, c, grouped[c])
                 for c in passes:
                     for acc, cols in zip(accs, column_tiles):
                         multiply(gate, c, acc, cols)
                 for acc, cols in zip(accs, column_tiles):
-                    store(gate, 1.0, acc, cols)
+                    store(gate, sign, acc, cols)
 
             d_banks = [psum.tile([P, PACK, P], F32, name="d_bank", tag="d_bank") for cols in column_tiles]
             for d_bank, cols in zip(d_banks, column_tiles):
@@ -187,12 +196,8 @@ def tile_grouptorchgru_v_kernel(
                 )
 
             one_behind(half_passes, make_m, make_mz)
-            for c in passes:
-                nc.vector.quantize_mx(
-                    out=x_codes[:, c, :].bitcast(E4M3_X4),
-                    scales=x_scales[:, c, :],
-                    in_=x_grouped[c][:].rearrange("p w j -> p (w j)"),
-                )
+            if u > 0:
+                quantise_x(u)
 
             d_rows = [sbuf.tile([P, PACK, H], F32, name="d%d" % c) for c in passes[:-1]]
             for c in passes[:-1]:
@@ -205,9 +210,13 @@ def tile_grouptorchgru_v_kernel(
                     op0=ALU.subtract, op1=ALU.mult,
                 )
                 nc.scalar.copy(out=grouped_by_runs(dn_grouped[c]), in_=by_runs(dn[c]))
-            hrr = rows_per_pass("hrr", F32)
+            hrr = r
             for c in passes:
                 nc.scalar.activation(out=flat(hrr[c]), in_=flat(r[c]), func=ACT.Square, bias=-0.5)
+            if u == 0:
+                for v in units:
+                    for c in passes:
+                        nc.scalar.copy(out=grouped_by_runs(x_grouped[v][c]), in_=by_runs(x[c][:, :, v, :]))
 
             dz_grouped = grouped_per_pass("dz_grouped")
             for c in passes[:-1]:
@@ -223,21 +232,16 @@ def tile_grouptorchgru_v_kernel(
                     op=ALU.mult,
                 )
             if another_unit:
-                next_z_g_x_n_h = load_z_g_x_n_h(u + 1)
+                next_z_g_n_h = load_z_g_n_h(u + 1)
 
-            quantise_multiply_store(DN, dn_grouped)
-            quantise_multiply_store(DZ, dz_grouped)
-
-            for c in passes:
-                nc.vector.scalar_tensor_tensor(
-                    out=flat(hrr[c]), in0=flat(hrr[c]), scalar=0.25, in1=flat(hn_rows[c]),
-                    op0=ALU.subtract, op1=ALU.mult,
-                )
-            if another_unit:
-                next_r_hn = load_r_hn(u + 1)
+            def make_hrr():
+                for c in passes:
+                    nc.vector.scalar_tensor_tensor(
+                        out=flat(hrr[c]), in0=flat(hrr[c]), scalar=0.25, in1=flat(hn_rows[c]),
+                        op0=ALU.subtract, op1=ALU.mult,
+                    )
 
             dr_grouped = grouped_per_pass("dr_grouped")
-            dr_accs = open_banks()
 
             def make_dr(c, tiles):
                 cols = slice(tiles[0] * P, (tiles[-1] + 1) * P)
@@ -248,19 +252,40 @@ def tile_grouptorchgru_v_kernel(
                     op=ALU.mult,
                 )
 
-            def finish_dr(c, tiles):
-                quantise(DR, c, dr_grouped[c], slice(tiles[0] * P, (tiles[-1] + 1) * P))
-                for t in tiles:
-                    multiply(DR, c, dr_accs[t], column_tiles[t])
-                    if c == last_pass:
-                        store(DR, -1.0, dr_accs[t], column_tiles[t])
-
-            all_tiles = list(range(len(column_tiles)))
-            whole_passes = [(c, all_tiles) for c in passes[:-1]]
-            tiles_of_last_pass = [(last_pass, [t]) for t in all_tiles]
-            one_behind(whole_passes + tiles_of_last_pass, make_dr, finish_dr)
-
             if another_unit:
-                z, g, x, n, h = next_z_g_x_n_h
+                for gate, grouped in ((DN, dn_grouped), (DZ, dz_grouped)):
+                    for c in passes:
+                        quantise(gate, c, grouped[c])
+                make_hrr()
+                for c in passes:
+                    make_dr(c, all_tiles)
+                next_r_hn = load_r_hn(u + 1)
+                quantise_x(u)
+                for c in passes:
+                    quantise(DR, c, dr_grouped[c])
+                multiply_store(DN, 1.0)
+                multiply_store(DZ, 1.0)
+                multiply_store(DR, -1.0)
+
+                z, g, n, h = next_z_g_n_h
                 r, hn_rows = next_r_hn
-                x_grouped, dn = regroup_x_and_square_n(x, n)
+                dn = square_n(n)
+            else:
+                for gate, grouped in ((DN, dn_grouped), (DZ, dz_grouped)):
+                    for c in passes:
+                        quantise(gate, c, grouped[c])
+                    multiply_store(gate, 1.0)
+                make_hrr()
+
+                dr_accs = open_banks()
+
+                def finish_dr(c, tiles):
+                    quantise(DR, c, dr_grouped[c], slice(tiles[0] * P, (tiles[-1] + 1) * P))
+                    for t in tiles:
+                        multiply(DR, c, dr_accs[t], column_tiles[t])
+                        if c == last_pass:
+                            store(DR, -1.0, dr_accs[t], column_tiles[t])
+
+                whole_passes = [(c, all_tiles) for c in passes[:-1]]
+                tiles_of_last_pass = [(last_pass, [t]) for t in all_tiles]
+                one_behind(whole_passes + tiles_of_last_pass, make_dr, finish_dr)

@@ -17,6 +17,7 @@ P = 128
 PACK = 4
 K_PASS = P * PACK
 PASSES = B // K_PASS
+ROWS = PASSES * PACK
 TILES_OF_A_UNIT = GATES * H // P
 RUN = 4
 
@@ -25,23 +26,23 @@ BYTES = 2 * 3 * B * U * H + 4 * B * U * (GATES + 1) * H + 4 * U * GATES * H * I
 
 
 def flat(rows):
-    return rows[:].rearrange("p j w -> p (j w)")
+    return rows.rearrange("p j w -> p (j w)")
 
 
 def by_runs(rows):
-    return rows[:].rearrange("p j (c i) -> p c j i", i=RUN)
+    return rows.rearrange("p j (c i) -> p c j i", i=RUN)
 
 
 def grouped_by_runs(grouped):
-    return grouped[:].rearrange("p (c i) j -> p c j i", i=RUN)
+    return grouped.rearrange("p (c i) j -> p c j i", i=RUN)
 
 
 def one_behind(pieces, produce, consume):
     for i, piece in enumerate(pieces):
-        produce(*piece)
+        produce(piece)
         if i > 0:
-            consume(*pieces[i - 1])
-    consume(*pieces[-1])
+            consume(pieces[i - 1])
+    consume(pieces[-1])
 
 
 def tile_grouptorchgru_v_kernel(
@@ -51,10 +52,10 @@ def tile_grouptorchgru_v_kernel(
     passes = range(PASSES)
     units = range(U)
     last_pass = PASSES - 1
-    row_halves = [slice(j, j + PACK // 2) for j in range(0, PACK, PACK // 2)]
-    half_passes = [(c, rows) for c in passes for rows in row_halves]
+    rows_of_pass = [slice(c * PACK, (c + 1) * PACK) for c in passes]
     column_tiles = [slice(first, first + P) for first in range(0, H, P)]
     all_tiles = list(range(len(column_tiles)))
+    pieces_of_unit = [[slice(0, 1), slice(1, 2), slice(2, 4), slice(4, 6), slice(6, 8)]] + [rows_of_pass] * (U - 1)
 
     def by_pass(dram):
         return dram.rearrange("(c p j) u w -> c u p j w", c=PASSES, p=P, j=PACK)
@@ -63,7 +64,9 @@ def tile_grouptorchgru_v_kernel(
     h_dram = by_pass(hidden)
     g_dram = by_pass(grad_out)
     hn_dram = by_pass(hn)
-    gates_dram = gates.rearrange("(c p j) u (s w) -> s c u p j w", c=PASSES, p=P, j=PACK, s=GATES)
+    r_dram, z_dram, n_dram = [
+        by_pass(gates[:, :, s * H : (s + 1) * H]) for s in range(GATES)
+    ]
 
     with (
         tc.tile_pool(name="sbuf", bufs=1) as sbuf,
@@ -72,38 +75,39 @@ def tile_grouptorchgru_v_kernel(
         tc.manual_schedule(),
     ):
 
-        def rows_per_pass(name, dtype):
-            return [sbuf.tile([P, PACK, H], dtype, name="%s%d" % (name, c)) for c in passes]
+        def rows_tile(name, dtype):
+            return sbuf.tile([P, ROWS, H], dtype, name=name)
 
-        def grouped_per_pass(name):
-            return [
-                sbuf.tile([P, H, PACK], BF16, name="%s%d" % (name, c), align_bytes=64)
-                for c in passes
-            ]
+        def grouped_tile(name):
+            return sbuf.tile([P, PASSES, H, PACK], BF16, name=name, align_bytes=64)
+
+        def load(tile, dram, u, rows):
+            c = rows.start // PACK
+            in_pass = slice(rows.start - c * PACK, rows.stop - c * PACK)
+            nc.sync.dma_start(out=tile[:, rows, :], in_=dram[c, u][:, in_pass, :])
 
         def load_z_g_n_h(u):
-            z, n = [rows_per_pass(name, F32) for name in ("z", "n")]
-            g, h = [rows_per_pass(name, BF16) for name in ("g", "h")]
-            for c in passes:
-                for rows in row_halves:
-                    nc.sync.dma_start(out=z[c][:, rows, :], in_=gates_dram[1, c, u][:, rows, :])
-                    nc.sync.dma_start(out=g[c][:, rows, :], in_=g_dram[c, u][:, rows, :])
-            for c in passes:
-                nc.sync.dma_start(out=n[c][:], in_=gates_dram[2, c, u])
-                nc.sync.dma_start(out=h[c][:], in_=h_dram[c, u])
+            z, n = [rows_tile(name, F32) for name in ("z", "n")]
+            g, h = [rows_tile(name, BF16) for name in ("g", "h")]
+            for rows in pieces_of_unit[u]:
+                load(z, z_dram, u, rows)
+                load(g, g_dram, u, rows)
+            for rows in rows_of_pass:
+                load(n, n_dram, u, rows)
+                load(h, h_dram, u, rows)
             return z, g, n, h
 
         def load_r_hn(u):
-            r, hn_rows = [rows_per_pass(name, F32) for name in ("r", "hn")]
-            for c in passes:
-                nc.sync.dma_start(out=r[c][:], in_=gates_dram[0, c, u])
-                nc.sync.dma_start(out=hn_rows[c][:], in_=hn_dram[c, u])
+            r, hn_rows = [rows_tile(name, F32) for name in ("r", "hn")]
+            for rows in rows_of_pass:
+                load(r, r_dram, u, rows)
+                load(hn_rows, hn_dram, u, rows)
             return r, hn_rows
 
         def square_n(n):
-            dn = rows_per_pass("dn", F32)
-            for c in passes:
-                nc.scalar.activation(out=flat(dn[c]), in_=flat(n[c]), func=ACT.Square)
+            dn = rows_tile("dn", F32)
+            for rows in rows_of_pass:
+                nc.scalar.activation(out=flat(dn[:, rows, :]), in_=flat(n[:, rows, :]), func=ACT.Square)
             return dn
 
         identity = sbuf.tile([P, P], F32)
@@ -113,54 +117,61 @@ def tile_grouptorchgru_v_kernel(
 
         z, g, n, h = load_z_g_n_h(0)
         r, hn_rows = load_r_hn(0)
-        x = [sbuf.tile([P, PACK, U, I], BF16, name="x%d" % c) for c in passes]
+        x = sbuf.tile([P, PASSES, PACK, U, I], BF16)
         for c in passes:
-            nc.sync.dma_start(out=x[c][:], in_=x_dram[c])
+            nc.sync.dma_start(out=x[:, c, :, :, :], in_=x_dram[c])
         dn = square_n(n)
 
-        x_grouped = [grouped_per_pass("x_grouped_%d_" % u) for u in units]
+        x_grouped = [grouped_tile("x_grouped%d" % u) for u in units]
         x_codes = sbuf.tile([P, U, PASSES, I], U32, align_bytes=64)
         x_scales = sbuf.tile([P, U, PASSES, I], U8, align_bytes=64)
 
         def quantise_x(u):
-            for c in passes:
-                nc.vector.quantize_mx(
-                    out=x_codes[:, u, c, :].bitcast(E4M3_X4),
-                    scales=x_scales[:, u, c, :],
-                    in_=x_grouped[u][c][:].rearrange("p w j -> p (w j)"),
-                )
+            nc.vector.quantize_mx(
+                out=x_codes[:, u, :, :].rearrange("p c w -> p (c w)").bitcast(E4M3_X4),
+                scales=x_scales[:, u, :, :].rearrange("p c w -> p (c w)"),
+                in_=x_grouped[u][:].rearrange("p c w j -> p (c w j)"),
+            )
 
         for u in units:
             another_unit = u + 1 < U
-            dgx_codes = sbuf.tile([P, PASSES, GATES * H], U32, align_bytes=64)
-            dgx_scales = sbuf.tile([P, PASSES, GATES * H], U8, align_bytes=64)
+            dgx_codes = sbuf.tile([P, GATES, PASSES, H], U32, align_bytes=64)
+            dgx_scales = sbuf.tile([P, GATES, PASSES, H], U8, align_bytes=64)
 
-            def quantise(gate, c, grouped, cols=slice(0, H)):
-                first = gate * H
+            def quantise_gate(gate, grouped):
                 nc.vector.quantize_mx(
-                    out=dgx_codes[:, c, first:][:, cols].bitcast(E5M2_X4),
-                    scales=dgx_scales[:, c, first:][:, cols],
-                    in_=grouped[:, cols, :].rearrange("p w j -> p (w j)"),
+                    out=dgx_codes[:, gate, :, :].rearrange("p c w -> p (c w)").bitcast(E5M2_X4),
+                    scales=dgx_scales[:, gate, :, :].rearrange("p c w -> p (c w)"),
+                    in_=grouped[:].rearrange("p c w j -> p (c w j)"),
+                )
+
+            def quantise(gate, c, grouped, cols):
+                nc.vector.quantize_mx(
+                    out=dgx_codes[:, gate, c, cols].bitcast(E5M2_X4),
+                    scales=dgx_scales[:, gate, c, cols],
+                    in_=grouped[:, c, cols, :].rearrange("p w j -> p (w j)"),
                 )
 
             def open_banks():
                 return [psum.tile([P, I], F32, name="acc", tag="acc") for cols in column_tiles]
 
             def multiply(gate, c, acc, cols):
-                first = gate * H
                 nc.tensor.matmul_mx(
                     out=acc[:],
-                    lhsT=dgx_codes[:, c, first:][:, cols].bitcast(E5M2_X4),
-                    lhsT_scale=dgx_scales[:, c, first:][:, cols],
+                    lhsT=dgx_codes[:, gate, c, cols].bitcast(E5M2_X4),
+                    lhsT_scale=dgx_scales[:, gate, c, cols],
                     rhs=x_codes[:, u, c, :].bitcast(E4M3_X4),
                     rhs_scale=x_scales[:, u, c, :],
                     start=(c == 0),
                     stop=(c == last_pass),
                 )
 
-            def store(gate, sign, acc, cols):
+            def store(gate, sign, acc, cols, by_vector=False):
                 result = results.tile([P, I], F32)
-                nc.scalar.mul(out=result[:], in_=acc[:], mul=sign)
+                if by_vector:
+                    nc.vector.tensor_scalar_mul(out=result[:], in0=acc[:], scalar1=sign)
+                else:
+                    nc.scalar.mul(out=result[:], in_=acc[:], mul=sign)
                 nc.sync.dma_start(out=out[u, gate * H :, :][cols, :], in_=result[:])
 
             def multiply_store(gate, sign):
@@ -174,95 +185,101 @@ def tile_grouptorchgru_v_kernel(
             d_banks = [psum.tile([P, PACK, P], F32, name="d_bank", tag="d_bank") for cols in column_tiles]
             for d_bank, cols in zip(d_banks, column_tiles):
                 nc.tensor.matmul(
-                    out=d_bank[:], lhsT=identity[:], rhs=n[last_pass][:, :, cols], start=True, stop=False
+                    out=d_bank[:], lhsT=identity[:], rhs=n[:, rows_of_pass[last_pass], cols],
+                    start=True, stop=False,
                 )
                 nc.tensor.matmul(
-                    out=d_bank[:], lhsT=minus_identity[:], rhs=h[last_pass][:, :, cols], start=False, stop=True
+                    out=d_bank[:], lhsT=minus_identity[:], rhs=h[:, rows_of_pass[last_pass], cols],
+                    start=False, stop=True,
                 )
 
-            m = rows_per_pass("m", F32)
+            m = rows_tile("m", F32)
             mz = z
 
-            def make_m(c, rows):
+            def make_m(rows):
                 nc.vector.scalar_tensor_tensor(
-                    out=flat(m[c][:, rows, :]), in0=flat(z[c][:, rows, :]), scalar=1.0,
-                    in1=flat(g[c][:, rows, :]), op0=ALU.subtract, op1=ALU.mult,
+                    out=flat(m[:, rows, :]), in0=flat(z[:, rows, :]), scalar=1.0,
+                    in1=flat(g[:, rows, :]), op0=ALU.subtract, op1=ALU.mult,
                 )
 
-            def make_mz(c, rows):
+            def make_mz(rows):
                 nc.vector.tensor_tensor(
-                    out=flat(mz[c][:, rows, :]), in0=flat(m[c][:, rows, :]),
-                    in1=flat(z[c][:, rows, :]), op=ALU.mult,
+                    out=flat(mz[:, rows, :]), in0=flat(m[:, rows, :]),
+                    in1=flat(z[:, rows, :]), op=ALU.mult,
                 )
 
-            one_behind(half_passes, make_m, make_mz)
+            one_behind(pieces_of_unit[u], make_m, make_mz)
             if u > 0:
                 quantise_x(u)
 
-            d_rows = [sbuf.tile([P, PACK, H], F32, name="d%d" % c) for c in passes[:-1]]
-            for c in passes[:-1]:
-                nc.vector.tensor_tensor(out=flat(d_rows[c]), in0=flat(n[c]), in1=flat(h[c]), op=ALU.subtract)
+            d_rows = sbuf.tile([P, ROWS - PACK, H], F32)
+            for rows in rows_of_pass[:-1]:
+                nc.vector.tensor_tensor(
+                    out=flat(d_rows[:, rows, :]), in0=flat(n[:, rows, :]), in1=flat(h[:, rows, :]),
+                    op=ALU.subtract,
+                )
 
-            dn_grouped = grouped_per_pass("dn_grouped")
-            for c in passes:
+            dn_grouped = grouped_tile("dn_grouped")
+            for c, rows in enumerate(rows_of_pass):
                 nc.vector.scalar_tensor_tensor(
-                    out=flat(dn[c]), in0=flat(dn[c]), scalar=1.0, in1=flat(m[c]),
+                    out=flat(dn[:, rows, :]), in0=flat(dn[:, rows, :]), scalar=1.0, in1=flat(m[:, rows, :]),
                     op0=ALU.subtract, op1=ALU.mult,
                 )
-                nc.scalar.copy(out=grouped_by_runs(dn_grouped[c]), in_=by_runs(dn[c]))
+                nc.scalar.copy(out=grouped_by_runs(dn_grouped[:, c, :, :]), in_=by_runs(dn[:, rows, :]))
             hrr = r
-            for c in passes:
-                nc.scalar.activation(out=flat(hrr[c]), in_=flat(r[c]), func=ACT.Square, bias=-0.5)
+            for rows in rows_of_pass:
+                nc.scalar.activation(
+                    out=flat(hrr[:, rows, :]), in_=flat(r[:, rows, :]), func=ACT.Square, bias=-0.5
+                )
             if u == 0:
                 for v in units:
                     for c in passes:
-                        nc.scalar.copy(out=grouped_by_runs(x_grouped[v][c]), in_=by_runs(x[c][:, :, v, :]))
+                        nc.scalar.copy(out=grouped_by_runs(x_grouped[v][:, c, :, :]), in_=by_runs(x[:, c, :, v, :]))
 
-            dz_grouped = grouped_per_pass("dz_grouped")
-            for c in passes[:-1]:
+            dz_grouped = grouped_tile("dz_grouped")
+            for c, rows in enumerate(rows_of_pass[:-1]):
                 nc.vector.tensor_tensor(
-                    out=grouped_by_runs(dz_grouped[c]), in0=by_runs(mz[c]), in1=by_runs(d_rows[c]),
-                    op=ALU.mult,
+                    out=grouped_by_runs(dz_grouped[:, c, :, :]), in0=by_runs(mz[:, rows, :]),
+                    in1=by_runs(d_rows[:, rows, :]), op=ALU.mult,
                 )
             for d_bank, cols in zip(d_banks, column_tiles):
                 nc.vector.tensor_tensor(
-                    out=grouped_by_runs(dz_grouped[last_pass][:, cols, :]),
-                    in0=by_runs(mz[last_pass][:, :, cols]),
-                    in1=by_runs(d_bank),
+                    out=grouped_by_runs(dz_grouped[:, last_pass, cols, :]),
+                    in0=by_runs(mz[:, rows_of_pass[last_pass], cols]),
+                    in1=by_runs(d_bank[:]),
                     op=ALU.mult,
                 )
             if another_unit:
                 next_z_g_n_h = load_z_g_n_h(u + 1)
 
             def make_hrr():
-                for c in passes:
+                for rows in rows_of_pass:
                     nc.vector.scalar_tensor_tensor(
-                        out=flat(hrr[c]), in0=flat(hrr[c]), scalar=0.25, in1=flat(hn_rows[c]),
-                        op0=ALU.subtract, op1=ALU.mult,
+                        out=flat(hrr[:, rows, :]), in0=flat(hrr[:, rows, :]), scalar=0.25,
+                        in1=flat(hn_rows[:, rows, :]), op0=ALU.subtract, op1=ALU.mult,
                     )
 
-            dr_grouped = grouped_per_pass("dr_grouped")
+            dr_grouped = grouped_tile("dr_grouped")
 
-            def make_dr(c, tiles):
+            def make_dr(piece):
+                c, tiles = piece
                 cols = slice(tiles[0] * P, (tiles[-1] + 1) * P)
                 nc.vector.tensor_tensor(
-                    out=grouped_by_runs(dr_grouped[c][:, cols, :]),
-                    in0=by_runs(dn[c][:, :, cols]),
-                    in1=by_runs(hrr[c][:, :, cols]),
+                    out=grouped_by_runs(dr_grouped[:, c, cols, :]),
+                    in0=by_runs(dn[:, rows_of_pass[c], cols]),
+                    in1=by_runs(hrr[:, rows_of_pass[c], cols]),
                     op=ALU.mult,
                 )
 
             if another_unit:
-                for gate, grouped in ((DN, dn_grouped), (DZ, dz_grouped)):
-                    for c in passes:
-                        quantise(gate, c, grouped[c])
+                quantise_gate(DN, dn_grouped)
+                quantise_gate(DZ, dz_grouped)
                 make_hrr()
                 for c in passes:
-                    make_dr(c, all_tiles)
+                    make_dr((c, all_tiles))
                 next_r_hn = load_r_hn(u + 1)
                 quantise_x(u)
-                for c in passes:
-                    quantise(DR, c, dr_grouped[c])
+                quantise_gate(DR, dr_grouped)
                 multiply_store(DN, 1.0)
                 multiply_store(DZ, 1.0)
                 multiply_store(DR, -1.0)
@@ -271,16 +288,17 @@ def tile_grouptorchgru_v_kernel(
                 r, hn_rows = next_r_hn
                 dn = square_n(n)
             else:
-                for gate, grouped in ((DN, dn_grouped), (DZ, dz_grouped)):
-                    for c in passes:
-                        quantise(gate, c, grouped[c])
-                    multiply_store(gate, 1.0)
+                quantise_gate(DN, dn_grouped)
+                multiply_store(DN, 1.0)
+                quantise_gate(DZ, dz_grouped)
+                multiply_store(DZ, 1.0)
                 make_hrr()
 
                 dr_accs = open_banks()
 
-                def finish_dr(c, tiles):
-                    quantise(DR, c, dr_grouped[c], slice(tiles[0] * P, (tiles[-1] + 1) * P))
+                def finish_dr(piece):
+                    c, tiles = piece
+                    quantise(DR, c, dr_grouped, slice(tiles[0] * P, (tiles[-1] + 1) * P))
                     for t in tiles:
                         multiply(DR, c, dr_accs[t], column_tiles[t])
                         if c == last_pass:

@@ -55,7 +55,8 @@ def tile_grouptorchgru_v_kernel(
     rows_of_pass = [slice(c * PACK, (c + 1) * PACK) for c in passes]
     column_tiles = [slice(first, first + P) for first in range(0, H, P)]
     all_tiles = list(range(len(column_tiles)))
-    pieces_of_unit = [[slice(0, 1), slice(1, 2), slice(2, 4), slice(4, 6), slice(6, 8)]] + [rows_of_pass] * (U - 1)
+    half_passes = [slice(first, first + PACK // 2) for first in range(0, ROWS, PACK // 2)]
+    pieces_of_unit = [[slice(0, 1), slice(1, 2)] + half_passes[1:]] + [half_passes] * (U - 1)
 
     def by_pass(dram):
         return dram.rearrange("(c p j) u w -> c u p j w", c=PASSES, p=P, j=PACK)

@@ -19,7 +19,7 @@ K_PASS = P * PACK
 PASSES = B // K_PASS
 ROWS = PASSES * PACK
 TILES_OF_A_UNIT = GATES * H // P
-RUN = 4
+RUN = 8
 
 FLOPS = 2 * U * GATES * H * I * B
 BYTES = 2 * 3 * B * U * H + 4 * B * U * (GATES + 1) * H + 4 * U * GATES * H * I
@@ -56,7 +56,8 @@ def tile_grouptorchgru_v_kernel(
     column_tiles = [slice(first, first + P) for first in range(0, H, P)]
     all_tiles = list(range(len(column_tiles)))
     half_passes = [slice(first, first + PACK // 2) for first in range(0, ROWS, PACK // 2)]
-    pieces_of_unit = [[slice(0, 1), slice(1, 2)] + half_passes[1:]] + [half_passes] * (U - 1)
+    pieces_of_unit = [[slice(row, row + 1) for row in range(ROWS)]] + [half_passes] * (U - 1)
+    n_pieces_of_unit = [half_passes[: PACK // 2] + rows_of_pass[1:]] + [rows_of_pass] * (U - 1)
 
     def by_pass(dram):
         return dram.rearrange("(c p j) u w -> c u p j w", c=PASSES, p=P, j=PACK)
@@ -93,7 +94,7 @@ def tile_grouptorchgru_v_kernel(
             for rows in pieces_of_unit[u]:
                 load(z, z_dram, u, rows)
                 load(g, g_dram, u, rows)
-            for rows in rows_of_pass:
+            for rows in n_pieces_of_unit[u]:
                 load(n, n_dram, u, rows)
                 load(h, h_dram, u, rows)
             return z, g, n, h
@@ -105,9 +106,9 @@ def tile_grouptorchgru_v_kernel(
                 load(hn_rows, hn_dram, u, rows)
             return r, hn_rows
 
-        def square_n(n):
+        def square_n(u, n):
             dn = rows_tile("dn", F32)
-            for rows in rows_of_pass:
+            for rows in n_pieces_of_unit[u]:
                 nc.scalar.activation(out=flat(dn[:, rows, :]), in_=flat(n[:, rows, :]), func=ACT.Square)
             return dn
 
@@ -115,13 +116,15 @@ def tile_grouptorchgru_v_kernel(
         make_identity(nc, identity[:])
         minus_identity = sbuf.tile([P, P], BF16)
         nc.scalar.mul(out=minus_identity[:], in_=identity[:], mul=-1.0)
+        first_square = sbuf.tile([P, 1], F32)
+        nc.scalar.activation(out=first_square[:], in_=identity[:, 0:1], func=ACT.Square)
 
         z, g, n, h = load_z_g_n_h(0)
         r, hn_rows = load_r_hn(0)
         x = sbuf.tile([P, PASSES, PACK, U, I], BF16)
         for c in passes:
             nc.sync.dma_start(out=x[:, c, :, :, :], in_=x_dram[c])
-        dn = square_n(n)
+        dn = square_n(0, n)
 
         x_grouped = [grouped_tile("x_grouped%d" % u) for u in units]
         x_codes = sbuf.tile([P, U, PASSES, I], U32, align_bytes=64)
@@ -175,13 +178,19 @@ def tile_grouptorchgru_v_kernel(
                     nc.scalar.mul(out=result[:], in_=acc[:], mul=sign)
                 nc.sync.dma_start(out=out[u, gate * H :, :][cols, :], in_=result[:])
 
-            def multiply_store(gate, sign):
+            def multiply_all(gate):
                 accs = open_banks()
                 for c in passes:
                     for acc, cols in zip(accs, column_tiles):
                         multiply(gate, c, acc, cols)
+                return accs
+
+            def store_all(gate, sign, accs):
                 for acc, cols in zip(accs, column_tiles):
                     store(gate, sign, acc, cols)
+
+            def multiply_store(gate, sign):
+                store_all(gate, sign, multiply_all(gate))
 
             d_banks = [psum.tile([P, PACK, P], F32, name="d_bank", tag="d_bank") for cols in column_tiles]
             for d_bank, cols in zip(d_banks, column_tiles):
@@ -214,19 +223,25 @@ def tile_grouptorchgru_v_kernel(
                 quantise_x(u)
 
             d_rows = sbuf.tile([P, ROWS - PACK, H], F32)
-            for rows in rows_of_pass[:-1]:
+            for rows in n_pieces_of_unit[u][:-1]:
                 nc.vector.tensor_tensor(
                     out=flat(d_rows[:, rows, :]), in0=flat(n[:, rows, :]), in1=flat(h[:, rows, :]),
                     op=ALU.subtract,
                 )
 
             dn_grouped = grouped_tile("dn_grouped")
+            dz_grouped = grouped_tile("dz_grouped")
             for c, rows in enumerate(rows_of_pass):
                 nc.vector.scalar_tensor_tensor(
                     out=flat(dn[:, rows, :]), in0=flat(dn[:, rows, :]), scalar=1.0, in1=flat(m[:, rows, :]),
                     op0=ALU.subtract, op1=ALU.mult,
                 )
                 nc.scalar.copy(out=grouped_by_runs(dn_grouped[:, c, :, :]), in_=by_runs(dn[:, rows, :]))
+                if c < last_pass:
+                    nc.vector.tensor_tensor(
+                        out=grouped_by_runs(dz_grouped[:, c, :, :]), in0=by_runs(mz[:, rows, :]),
+                        in1=by_runs(d_rows[:, rows, :]), op=ALU.mult,
+                    )
             hrr = r
             for rows in rows_of_pass:
                 nc.scalar.activation(
@@ -237,12 +252,6 @@ def tile_grouptorchgru_v_kernel(
                     for c in passes:
                         nc.scalar.copy(out=grouped_by_runs(x_grouped[v][:, c, :, :]), in_=by_runs(x[:, c, :, v, :]))
 
-            dz_grouped = grouped_tile("dz_grouped")
-            for c, rows in enumerate(rows_of_pass[:-1]):
-                nc.vector.tensor_tensor(
-                    out=grouped_by_runs(dz_grouped[:, c, :, :]), in0=by_runs(mz[:, rows, :]),
-                    in1=by_runs(d_rows[:, rows, :]), op=ALU.mult,
-                )
             for d_bank, cols in zip(d_banks, column_tiles):
                 nc.vector.tensor_tensor(
                     out=grouped_by_runs(dz_grouped[:, last_pass, cols, :]),
@@ -283,11 +292,12 @@ def tile_grouptorchgru_v_kernel(
                 quantise_gate(DR, dr_grouped)
                 multiply_store(DN, 1.0)
                 multiply_store(DZ, 1.0)
-                multiply_store(DR, -1.0)
+                dr_accs = multiply_all(DR)
 
                 z, g, n, h = next_z_g_n_h
                 r, hn_rows = next_r_hn
-                dn = square_n(n)
+                dn = square_n(u + 1, n)
+                store_all(DR, -1.0, dr_accs)
             else:
                 quantise_gate(DN, dn_grouped)
                 multiply_store(DN, 1.0)

@@ -192,16 +192,16 @@ def tile_grouptorchgru_v_kernel(
             def multiply_store(gate, sign):
                 store_all(gate, sign, multiply_all(gate))
 
-            d_banks = [psum.tile([P, PACK, P], F32, name="d_bank", tag="d_bank") for cols in column_tiles]
-            for d_bank, cols in zip(d_banks, column_tiles):
-                nc.tensor.matmul(
-                    out=d_bank[:], lhsT=identity[:], rhs=n[:, rows_of_pass[last_pass], cols],
-                    start=True, stop=False,
-                )
-                nc.tensor.matmul(
-                    out=d_bank[:], lhsT=minus_identity[:], rhs=h[:, rows_of_pass[last_pass], cols],
-                    start=False, stop=True,
-                )
+            def subtract_in_psum(rows, cols):
+                d_bank = psum.tile([P, PACK, P], F32, name="d_bank", tag="d_bank")
+                nc.tensor.matmul(out=d_bank[:], lhsT=identity[:], rhs=n[:, rows, cols], start=True, stop=False)
+                nc.tensor.matmul(out=d_bank[:], lhsT=minus_identity[:], rhs=h[:, rows, cols], start=False, stop=True)
+                return d_bank
+
+            vector_cols = slice(0, H - P if another_unit else H)
+            extra_cols = slice(vector_cols.stop, H)
+            extra_banks = [subtract_in_psum(rows_of_pass[0], extra_cols)] if another_unit else []
+            d_banks = [subtract_in_psum(rows_of_pass[last_pass], cols) for cols in column_tiles]
 
             m = rows_tile("m", F32)
             mz = z
@@ -225,23 +225,36 @@ def tile_grouptorchgru_v_kernel(
             d_rows = sbuf.tile([P, ROWS - PACK, H], F32)
             for rows in n_pieces_of_unit[u][:-1]:
                 nc.vector.tensor_tensor(
-                    out=flat(d_rows[:, rows, :]), in0=flat(n[:, rows, :]), in1=flat(h[:, rows, :]),
+                    out=d_rows[:, rows, vector_cols], in0=n[:, rows, vector_cols], in1=h[:, rows, vector_cols],
                     op=ALU.subtract,
                 )
 
             dn_grouped = grouped_tile("dn_grouped")
             dz_grouped = grouped_tile("dz_grouped")
+
+            def make_dz_from_sbuf(c):
+                rows = rows_of_pass[c]
+                nc.vector.tensor_tensor(
+                    out=grouped_by_runs(dz_grouped[:, c, vector_cols, :]), in0=by_runs(mz[:, rows, vector_cols]),
+                    in1=by_runs(d_rows[:, rows, vector_cols]), op=ALU.mult,
+                )
+                for d_bank in extra_banks:
+                    nc.vector.tensor_tensor(
+                        out=grouped_by_runs(dz_grouped[:, c, extra_cols, :]), in0=by_runs(mz[:, rows, extra_cols]),
+                        in1=by_runs(d_bank[:]), op=ALU.mult,
+                    )
+
             for c, rows in enumerate(rows_of_pass):
                 nc.vector.scalar_tensor_tensor(
                     out=flat(dn[:, rows, :]), in0=flat(dn[:, rows, :]), scalar=1.0, in1=flat(m[:, rows, :]),
                     op0=ALU.subtract, op1=ALU.mult,
                 )
                 nc.scalar.copy(out=grouped_by_runs(dn_grouped[:, c, :, :]), in_=by_runs(dn[:, rows, :]))
-                if c < last_pass:
-                    nc.vector.tensor_tensor(
-                        out=grouped_by_runs(dz_grouped[:, c, :, :]), in0=by_runs(mz[:, rows, :]),
-                        in1=by_runs(d_rows[:, rows, :]), op=ALU.mult,
-                    )
+                if another_unit and c < last_pass:
+                    make_dz_from_sbuf(c)
+            if not another_unit:
+                for c in passes[:-1]:
+                    make_dz_from_sbuf(c)
             hrr = r
             for rows in rows_of_pass:
                 nc.scalar.activation(

@@ -19,6 +19,7 @@ K_PASS = P * PACK
 PASSES = B // K_PASS
 ROWS = PASSES * PACK
 TILES_OF_A_UNIT = GATES * H // P
+GPSIMD_COLUMNS = 160
 RUN = 8
 
 FLOPS = 2 * U * GATES * H * I * B
@@ -198,7 +199,7 @@ def tile_grouptorchgru_v_kernel(
                 nc.tensor.matmul(out=d_bank[:], lhsT=minus_identity[:], rhs=h[:, rows, cols], start=False, stop=True)
                 return d_bank
 
-            vector_cols = slice(0, H - P if another_unit else H)
+            vector_cols = slice(0, H - P if another_unit else H - GPSIMD_COLUMNS)
             extra_cols = slice(vector_cols.stop, H)
             extra_banks = [subtract_in_psum(rows_of_pass[0], extra_cols)] if another_unit else []
             d_banks = [subtract_in_psum(rows_of_pass[last_pass], cols) for cols in column_tiles]
@@ -255,6 +256,11 @@ def tile_grouptorchgru_v_kernel(
             if not another_unit:
                 for c in passes[:-1]:
                     make_dz_from_sbuf(c)
+                d_late = sbuf.tile([P, PACK, GPSIMD_COLUMNS], F32, name="d_late", tag="d_rows")
+                nc.gpsimd.tensor_tensor(
+                    out=d_late[:], in0=n[:, rows_of_pass[0], extra_cols], in1=h[:, rows_of_pass[0], extra_cols],
+                    op=ALU.subtract,
+                )
             hrr = r
             for rows in rows_of_pass:
                 nc.scalar.activation(
@@ -274,6 +280,13 @@ def tile_grouptorchgru_v_kernel(
                 )
             if another_unit:
                 next_z_g_n_h = load_z_g_n_h(u + 1)
+            else:
+                nc.vector.tensor_tensor(
+                    out=grouped_by_runs(dz_grouped[:, 0, extra_cols, :]),
+                    in0=by_runs(mz[:, rows_of_pass[0], extra_cols]),
+                    in1=by_runs(d_late[:]),
+                    op=ALU.mult,
+                )
 
             def make_hrr():
                 for rows in rows_of_pass:

@@ -20,6 +20,7 @@ PASSES = B // K_PASS
 ROWS = PASSES * PACK
 TILES_OF_A_UNIT = GATES * H // P
 GPSIMD_COLUMNS = 160
+AHEAD = 2
 RUN = 8
 
 FLOPS = 2 * U * GATES * H * I * B
@@ -336,10 +337,15 @@ def tile_grouptorchgru_v_kernel(
                 def finish_dr(piece):
                     c, tiles = piece
                     quantise(DR, c, dr_grouped, slice(tiles[0] * P, (tiles[-1] + 1) * P))
-                    for t in tiles:
-                        multiply(DR, c, dr_accs[t], column_tiles[t])
-                        if c == last_pass:
+                    if c < last_pass:
+                        for t in tiles[:AHEAD]:
+                            multiply(DR, c, dr_accs[t], column_tiles[t])
+                    else:
+                        for t in tiles:
+                            multiply(DR, c, dr_accs[t], column_tiles[t])
                             store(DR, -1.0, dr_accs[t], column_tiles[t])
+                            if t + AHEAD < len(column_tiles):
+                                multiply(DR, 0, dr_accs[t + AHEAD], column_tiles[t + AHEAD])
 
                 whole_passes = [(c, all_tiles) for c in passes[:-1]]
                 tiles_of_last_pass = [(last_pass, [t]) for t in all_tiles]

@@ -19,7 +19,7 @@ K_PASS = P * PACK
 PASSES = B // K_PASS
 ROWS = PASSES * PACK
 TILES_OF_A_UNIT = GATES * H // P
-GPSIMD_COLUMNS = 160
+GPSIMD_COLUMNS = 200
 AHEAD = 2
 RUN = 8
 
@@ -194,16 +194,17 @@ def tile_grouptorchgru_v_kernel(
             def multiply_store(gate, sign):
                 store_all(gate, sign, multiply_all(gate))
 
-            def subtract_in_psum(rows, cols):
-                d_bank = psum.tile([P, PACK, P], F32, name="d_bank", tag="d_bank")
+            def subtract_in_psum(rows, cols, tag="d_bank"):
+                d_bank = psum.tile([P, PACK, P], F32, name="d_bank", tag=tag)
                 nc.tensor.matmul(out=d_bank[:], lhsT=identity[:], rhs=n[:, rows, cols], start=True, stop=False)
                 nc.tensor.matmul(out=d_bank[:], lhsT=minus_identity[:], rhs=h[:, rows, cols], start=False, stop=True)
                 return d_bank
 
-            vector_cols = slice(0, H - P if another_unit else H - GPSIMD_COLUMNS)
-            extra_cols = slice(vector_cols.stop, H)
-            extra_banks = [subtract_in_psum(rows_of_pass[0], extra_cols)] if another_unit else []
+            vector_cols = slice(0, H if another_unit else H - GPSIMD_COLUMNS - P)
+            bank_cols = slice(vector_cols.stop, vector_cols.stop + (0 if another_unit else P))
+            extra_cols = slice(bank_cols.stop, H)
             d_banks = [subtract_in_psum(rows_of_pass[last_pass], cols) for cols in column_tiles]
+            extra_banks = [] if another_unit else [subtract_in_psum(rows_of_pass[0], bank_cols, tag="acc")]
 
             m = rows_tile("m", F32)
             mz = z
@@ -220,16 +221,29 @@ def tile_grouptorchgru_v_kernel(
                     in1=flat(z[:, rows, :]), op=ALU.mult,
                 )
 
-            one_behind(pieces_of_unit[u], make_m, make_mz)
+            if another_unit:
+                make_m(pieces_of_unit[u][0])
+                make_mz(pieces_of_unit[u][0])
+                one_behind(pieces_of_unit[u][1:], make_m, make_mz)
+            else:
+                one_behind(pieces_of_unit[u], make_m, make_mz)
             if u > 0:
                 quantise_x(u)
 
             d_rows = sbuf.tile([P, ROWS - PACK, H], F32)
+            def make_dn(rows):
+                nc.vector.scalar_tensor_tensor(
+                    out=flat(dn[:, rows, :]), in0=flat(dn[:, rows, :]), scalar=1.0, in1=flat(m[:, rows, :]),
+                    op0=ALU.subtract, op1=ALU.mult,
+                )
+
             for rows in n_pieces_of_unit[u][:-1]:
                 nc.vector.tensor_tensor(
                     out=d_rows[:, rows, vector_cols], in0=n[:, rows, vector_cols], in1=h[:, rows, vector_cols],
                     op=ALU.subtract,
                 )
+                if another_unit:
+                    make_dn(rows)
 
             dn_grouped = grouped_tile("dn_grouped")
             dz_grouped = grouped_tile("dz_grouped")
@@ -240,17 +254,10 @@ def tile_grouptorchgru_v_kernel(
                     out=grouped_by_runs(dz_grouped[:, c, vector_cols, :]), in0=by_runs(mz[:, rows, vector_cols]),
                     in1=by_runs(d_rows[:, rows, vector_cols]), op=ALU.mult,
                 )
-                for d_bank in extra_banks:
-                    nc.vector.tensor_tensor(
-                        out=grouped_by_runs(dz_grouped[:, c, extra_cols, :]), in0=by_runs(mz[:, rows, extra_cols]),
-                        in1=by_runs(d_bank[:]), op=ALU.mult,
-                    )
 
             for c, rows in enumerate(rows_of_pass):
-                nc.vector.scalar_tensor_tensor(
-                    out=flat(dn[:, rows, :]), in0=flat(dn[:, rows, :]), scalar=1.0, in1=flat(m[:, rows, :]),
-                    op0=ALU.subtract, op1=ALU.mult,
-                )
+                if not (another_unit and c < last_pass):
+                    make_dn(rows)
                 nc.scalar.copy(out=grouped_by_runs(dn_grouped[:, c, :, :]), in_=by_runs(dn[:, rows, :]))
                 if another_unit and c < last_pass:
                     make_dz_from_sbuf(c)
@@ -278,6 +285,11 @@ def tile_grouptorchgru_v_kernel(
                     in0=by_runs(mz[:, rows_of_pass[last_pass], cols]),
                     in1=by_runs(d_bank[:]),
                     op=ALU.mult,
+                )
+            for d_bank in extra_banks:
+                nc.vector.tensor_tensor(
+                    out=grouped_by_runs(dz_grouped[:, 0, bank_cols, :]), in0=by_runs(mz[:, rows_of_pass[0], bank_cols]),
+                    in1=by_runs(d_bank[:]), op=ALU.mult,
                 )
             if another_unit:
                 next_z_g_n_h = load_z_g_n_h(u + 1)

@@ -19,7 +19,8 @@ K_PASS = P * PACK
 PASSES = B // K_PASS
 ROWS = PASSES * PACK
 TILES_OF_A_UNIT = GATES * H // P
-GPSIMD_COLUMNS = 200
+GPSIMD_COLUMNS = 256
+MOVED = 2
 AHEAD = 2
 RUN = 8
 
@@ -200,11 +201,16 @@ def tile_grouptorchgru_v_kernel(
                 nc.tensor.matmul(out=d_bank[:], lhsT=minus_identity[:], rhs=h[:, rows, cols], start=False, stop=True)
                 return d_bank
 
-            vector_cols = slice(0, H if another_unit else H - GPSIMD_COLUMNS - P)
-            bank_cols = slice(vector_cols.stop, vector_cols.stop + (0 if another_unit else P))
-            extra_cols = slice(bank_cols.stop, H)
-            d_banks = [subtract_in_psum(rows_of_pass[last_pass], cols) for cols in column_tiles]
-            extra_banks = [] if another_unit else [subtract_in_psum(rows_of_pass[0], bank_cols, tag="acc")]
+            vector_cols = slice(0, H if another_unit else H - GPSIMD_COLUMNS - MOVED * P)
+            bank_cols = [] if another_unit else [slice(vector_cols.stop + i * P, vector_cols.stop + (i + 1) * P) for i in range(MOVED)]
+            extra_cols = slice(vector_cols.stop + len(bank_cols) * P, H)
+            tensor_tiles = column_tiles[: len(column_tiles) - (MOVED - 1)] if another_unit else column_tiles
+            vector_tiles = column_tiles[len(tensor_tiles) :]
+            extra_banks = [subtract_in_psum(rows_of_pass[0], cols) for cols in bank_cols]
+            d_banks = [
+                subtract_in_psum(rows_of_pass[last_pass], cols, tag="d_bank" if i + len(bank_cols) < 4 else "acc")
+                for i, cols in enumerate(tensor_tiles)
+            ]
 
             m = rows_tile("m", F32)
             mz = z
@@ -230,7 +236,7 @@ def tile_grouptorchgru_v_kernel(
             if u > 0:
                 quantise_x(u)
 
-            d_rows = sbuf.tile([P, ROWS - PACK, H], F32)
+            d_rows = sbuf.tile([P, ROWS - PACK, H], F32, name="d_rows") if vector_cols.stop > 0 else None
             def make_dn(rows):
                 nc.vector.scalar_tensor_tensor(
                     out=flat(dn[:, rows, :]), in0=flat(dn[:, rows, :]), scalar=1.0, in1=flat(m[:, rows, :]),
@@ -238,10 +244,11 @@ def tile_grouptorchgru_v_kernel(
                 )
 
             for rows in n_pieces_of_unit[u][:-1]:
-                nc.vector.tensor_tensor(
-                    out=d_rows[:, rows, vector_cols], in0=n[:, rows, vector_cols], in1=h[:, rows, vector_cols],
-                    op=ALU.subtract,
-                )
+                if vector_cols.stop > 0:
+                    nc.vector.tensor_tensor(
+                        out=d_rows[:, rows, vector_cols], in0=n[:, rows, vector_cols], in1=h[:, rows, vector_cols],
+                        op=ALU.subtract,
+                    )
                 if another_unit:
                     make_dn(rows)
 
@@ -250,10 +257,11 @@ def tile_grouptorchgru_v_kernel(
 
             def make_dz_from_sbuf(c):
                 rows = rows_of_pass[c]
-                nc.vector.tensor_tensor(
-                    out=grouped_by_runs(dz_grouped[:, c, vector_cols, :]), in0=by_runs(mz[:, rows, vector_cols]),
-                    in1=by_runs(d_rows[:, rows, vector_cols]), op=ALU.mult,
-                )
+                if vector_cols.stop > 0:
+                    nc.vector.tensor_tensor(
+                        out=grouped_by_runs(dz_grouped[:, c, vector_cols, :]), in0=by_runs(mz[:, rows, vector_cols]),
+                        in1=by_runs(d_rows[:, rows, vector_cols]), op=ALU.mult,
+                    )
 
             for c, rows in enumerate(rows_of_pass):
                 if not (another_unit and c < last_pass):
@@ -264,7 +272,7 @@ def tile_grouptorchgru_v_kernel(
             if not another_unit:
                 for c in passes[:-1]:
                     make_dz_from_sbuf(c)
-                d_late = sbuf.tile([P, PACK, GPSIMD_COLUMNS], F32, name="d_late", tag="d_rows")
+                d_late = sbuf.tile([P, PACK, GPSIMD_COLUMNS], F32, name="d_late", tag="m")
                 nc.gpsimd.tensor_tensor(
                     out=d_late[:], in0=n[:, rows_of_pass[0], extra_cols], in1=h[:, rows_of_pass[0], extra_cols],
                     op=ALU.subtract,
@@ -279,17 +287,30 @@ def tile_grouptorchgru_v_kernel(
                     for c in passes:
                         nc.scalar.copy(out=grouped_by_runs(x_grouped[v][:, c, :, :]), in_=by_runs(x[:, c, :, v, :]))
 
-            for d_bank, cols in zip(d_banks, column_tiles):
+            for d_bank, cols in zip(extra_banks, bank_cols):
+                nc.vector.tensor_tensor(
+                    out=grouped_by_runs(dz_grouped[:, 0, cols, :]), in0=by_runs(mz[:, rows_of_pass[0], cols]),
+                    in1=by_runs(d_bank[:]), op=ALU.mult,
+                )
+            d_more = sbuf.tile([P, PACK, P], F32, name="d_more") if vector_tiles else None
+            for cols in vector_tiles:
+                nc.vector.tensor_tensor(
+                    out=d_more[:], in0=n[:, rows_of_pass[last_pass], cols], in1=h[:, rows_of_pass[last_pass], cols],
+                    op=ALU.subtract,
+                )
+            for d_bank, cols in zip(d_banks, tensor_tiles):
                 nc.vector.tensor_tensor(
                     out=grouped_by_runs(dz_grouped[:, last_pass, cols, :]),
                     in0=by_runs(mz[:, rows_of_pass[last_pass], cols]),
                     in1=by_runs(d_bank[:]),
                     op=ALU.mult,
                 )
-            for d_bank in extra_banks:
+            for cols in vector_tiles:
                 nc.vector.tensor_tensor(
-                    out=grouped_by_runs(dz_grouped[:, 0, bank_cols, :]), in0=by_runs(mz[:, rows_of_pass[0], bank_cols]),
-                    in1=by_runs(d_bank[:]), op=ALU.mult,
+                    out=grouped_by_runs(dz_grouped[:, last_pass, cols, :]),
+                    in0=by_runs(mz[:, rows_of_pass[last_pass], cols]),
+                    in1=by_runs(d_more[:]),
+                    op=ALU.mult,
                 )
             if another_unit:
                 next_z_g_n_h = load_z_g_n_h(u + 1)

import concourse.mybir as mybir
from concourse.masks import make_identity

F32 = mybir.dt.float32
BF16 = mybir.dt.bfloat16
U32 = mybir.dt.uint32
U8 = mybir.dt.uint8
E4M3_X4 = mybir.dt.float8_e4m3fn_x4
E5M2_X4 = mybir.dt.float8_e5m2_x4
ALU = mybir.AluOpType
ACT = mybir.ActivationFunctionType

B, U, I, H = 1024, 2, 512, 512
GATES = 3
DR, DZ, DN = 0, 1, 2
P = 128
PACK = 4
K_PASS = P * PACK
PASSES = B // K_PASS
ROWS = PASSES * PACK
TILES_OF_A_UNIT = GATES * H // P
GPSIMD_COLUMNS = 256
MOVED = 2
AHEAD = 2
RUN = 8

FLOPS = 2 * U * GATES * H * I * B
BYTES = 2 * 3 * B * U * H + 4 * B * U * (GATES + 1) * H + 4 * U * GATES * H * I


def flat(rows):
    return rows.rearrange("p j w -> p (j w)")


def by_runs(rows):
    return rows.rearrange("p j (c i) -> p c j i", i=RUN)


def grouped_by_runs(grouped):
    return grouped.rearrange("p (c i) j -> p c j i", i=RUN)


def one_behind(pieces, produce, consume):
    for i, piece in enumerate(pieces):
        produce(piece)
        if i > 0:
            consume(pieces[i - 1])
    consume(pieces[-1])


def tile_grouptorchgru_v_kernel(
    tc, inputs, hidden, w_ih, w_hh, b_ih, b_hh, gates, hn, grad_out, out
):
    nc = tc.nc
    passes = range(PASSES)
    units = range(U)
    last_pass = PASSES - 1
    rows_of_pass = [slice(c * PACK, (c + 1) * PACK) for c in passes]
    column_tiles = [slice(first, first + P) for first in range(0, H, P)]
    all_tiles = list(range(len(column_tiles)))
    half_passes = [slice(first, first + PACK // 2) for first in range(0, ROWS, PACK // 2)]
    pieces_of_unit = [[slice(row, row + 1) for row in range(ROWS)]] + [half_passes] * (U - 1)
    n_pieces_of_unit = [half_passes[: PACK // 2] + rows_of_pass[1:]] + [rows_of_pass] * (U - 1)

    def by_pass(dram):
        return dram.rearrange("(c p j) u w -> c u p j w", c=PASSES, p=P, j=PACK)

    x_dram = inputs.rearrange("(c p j) u w -> c p j u w", c=PASSES, p=P, j=PACK)
    h_dram = by_pass(hidden)
    g_dram = by_pass(grad_out)
    hn_dram = by_pass(hn)
    r_dram, z_dram, n_dram = [
        by_pass(gates[:, :, s * H : (s + 1) * H]) for s in range(GATES)
    ]

    with (
        tc.tile_pool(name="sbuf", bufs=1) as sbuf,
        tc.tile_pool(name="results", bufs=TILES_OF_A_UNIT) as results,
        tc.psum_pool(name="psum", bufs=4) as psum,
        tc.manual_schedule(),
    ):

        def rows_tile(name, dtype):
            return sbuf.tile([P, ROWS, H], dtype, name=name)

        def grouped_tile(name):
            return sbuf.tile([P, PASSES, H, PACK], BF16, name=name, align_bytes=64)

        def load(tile, dram, u, rows):
            c = rows.start // PACK
            in_pass = slice(rows.start - c * PACK, rows.stop - c * PACK)
            nc.sync.dma_start(out=tile[:, rows, :], in_=dram[c, u][:, in_pass, :])

        def load_z_g_n_h(u):
            z, n = [rows_tile(name, F32) for name in ("z", "n")]
            g, h = [rows_tile(name, BF16) for name in ("g", "h")]
            for rows in pieces_of_unit[u]:
                load(z, z_dram, u, rows)
                load(g, g_dram, u, rows)
            for rows in n_pieces_of_unit[u]:
                load(n, n_dram, u, rows)
                load(h, h_dram, u, rows)
            return z, g, n, h

        def load_r_hn(u):
            r, hn_rows = [rows_tile(name, F32) for name in ("r", "hn")]
            for rows in rows_of_pass:
                load(r, r_dram, u, rows)
                load(hn_rows, hn_dram, u, rows)
            return r, hn_rows

        def square_n(u, n):
            dn = rows_tile("dn", F32)
            for rows in n_pieces_of_unit[u]:
                nc.scalar.activation(out=flat(dn[:, rows, :]), in_=flat(n[:, rows, :]), func=ACT.Square)
            return dn

        identity = sbuf.tile([P, P], F32)
        make_identity(nc, identity[:])
        minus_identity = sbuf.tile([P, P], BF16)
        nc.scalar.mul(out=minus_identity[:], in_=identity[:], mul=-1.0)
        first_square = sbuf.tile([P, 1], F32)
        nc.scalar.activation(out=first_square[:], in_=identity[:, 0:1], func=ACT.Square)

        z, g, n, h = load_z_g_n_h(0)
        r, hn_rows = load_r_hn(0)
        x = sbuf.tile([P, PASSES, PACK, U, I], BF16)
        for c in passes:
            nc.sync.dma_start(out=x[:, c, :, :, :], in_=x_dram[c])
        dn = square_n(0, n)

        x_grouped = [grouped_tile("x_grouped%d" % u) for u in units]
        x_codes = sbuf.tile([P, U, PASSES, I], U32, align_bytes=64)
        x_scales = sbuf.tile([P, U, PASSES, I], U8, align_bytes=64)

        def quantise_x(u):
            nc.vector.quantize_mx(
                out=x_codes[:, u, :, :].rearrange("p c w -> p (c w)").bitcast(E4M3_X4),
                scales=x_scales[:, u, :, :].rearrange("p c w -> p (c w)"),
                in_=x_grouped[u][:].rearrange("p c w j -> p (c w j)"),
            )

        for u in units:
            another_unit = u + 1 < U
            dgx_codes = sbuf.tile([P, GATES, PASSES, H], U32, align_bytes=64)
            dgx_scales = sbuf.tile([P, GATES, PASSES, H], U8, align_bytes=64)

            def quantise_gate(gate, grouped):
                nc.vector.quantize_mx(
                    out=dgx_codes[:, gate, :, :].rearrange("p c w -> p (c w)").bitcast(E5M2_X4),
                    scales=dgx_scales[:, gate, :, :].rearrange("p c w -> p (c w)"),
                    in_=grouped[:].rearrange("p c w j -> p (c w j)"),
                )

            def quantise(gate, c, grouped, cols):
                nc.vector.quantize_mx(
                    out=dgx_codes[:, gate, c, cols].bitcast(E5M2_X4),
                    scales=dgx_scales[:, gate, c, cols],
                    in_=grouped[:, c, cols, :].rearrange("p w j -> p (w j)"),
                )

            def open_banks():
                return [psum.tile([P, I], F32, name="acc", tag="acc") for cols in column_tiles]

            def multiply(gate, c, acc, cols):
                nc.tensor.matmul_mx(
                    out=acc[:],
                    lhsT=dgx_codes[:, gate, c, cols].bitcast(E5M2_X4),
                    lhsT_scale=dgx_scales[:, gate, c, cols],
                    rhs=x_codes[:, u, c, :].bitcast(E4M3_X4),
                    rhs_scale=x_scales[:, u, c, :],
                    start=(c == 0),
                    stop=(c == last_pass),
                )

            def store(gate, sign, acc, cols, by_vector=False):
                result = results.tile([P, I], F32)
                if by_vector:
                    nc.vector.tensor_scalar_mul(out=result[:], in0=acc[:], scalar1=sign)
                else:
                    nc.scalar.mul(out=result[:], in_=acc[:], mul=sign)
                nc.sync.dma_start(out=out[u, gate * H :, :][cols, :], in_=result[:])

            def multiply_all(gate):
                accs = open_banks()
                for c in passes:
                    for acc, cols in zip(accs, column_tiles):
                        multiply(gate, c, acc, cols)
                return accs

            def store_all(gate, sign, accs):
                for acc, cols in zip(accs, column_tiles):
                    store(gate, sign, acc, cols)

            def multiply_store(gate, sign):
                store_all(gate, sign, multiply_all(gate))

            def subtract_in_psum(rows, cols, tag="d_bank"):
                d_bank = psum.tile([P, PACK, P], F32, name="d_bank", tag=tag)
                nc.tensor.matmul(out=d_bank[:], lhsT=identity[:], rhs=n[:, rows, cols], start=True, stop=False)
                nc.tensor.matmul(out=d_bank[:], lhsT=minus_identity[:], rhs=h[:, rows, cols], start=False, stop=True)
                return d_bank

            vector_cols = slice(0, H if another_unit else H - GPSIMD_COLUMNS - MOVED * P)
            bank_cols = [] if another_unit else [slice(vector_cols.stop + i * P, vector_cols.stop + (i + 1) * P) for i in range(MOVED)]
            extra_cols = slice(vector_cols.stop + len(bank_cols) * P, H)
            tensor_tiles = column_tiles[: len(column_tiles) - (MOVED - 1)] if another_unit else column_tiles
            vector_tiles = column_tiles[len(tensor_tiles) :]
            extra_banks = [subtract_in_psum(rows_of_pass[0], cols) for cols in bank_cols]
            d_banks = [
                subtract_in_psum(rows_of_pass[last_pass], cols, tag="d_bank" if i + len(bank_cols) < 4 else "acc")
                for i, cols in enumerate(tensor_tiles)
            ]

            m = rows_tile("m", F32)
            mz = z

            def make_m(rows):
                nc.vector.scalar_tensor_tensor(
                    out=flat(m[:, rows, :]), in0=flat(z[:, rows, :]), scalar=1.0,
                    in1=flat(g[:, rows, :]), op0=ALU.subtract, op1=ALU.mult,
                )

            def make_mz(rows):
                nc.vector.tensor_tensor(
                    out=flat(mz[:, rows, :]), in0=flat(m[:, rows, :]),
                    in1=flat(z[:, rows, :]), op=ALU.mult,
                )

            if another_unit:
                make_m(pieces_of_unit[u][0])
                make_mz(pieces_of_unit[u][0])
                one_behind(pieces_of_unit[u][1:], make_m, make_mz)
            else:
                one_behind(pieces_of_unit[u], make_m, make_mz)
            if u > 0:
                quantise_x(u)

            d_rows = sbuf.tile([P, ROWS - PACK, H], F32, name="d_rows") if vector_cols.stop > 0 else None
            def make_dn(rows):
                nc.vector.scalar_tensor_tensor(
                    out=flat(dn[:, rows, :]), in0=flat(dn[:, rows, :]), scalar=1.0, in1=flat(m[:, rows, :]),
                    op0=ALU.subtract, op1=ALU.mult,
                )

            for rows in n_pieces_of_unit[u][:-1]:
                if vector_cols.stop > 0:
                    nc.vector.tensor_tensor(
                        out=d_rows[:, rows, vector_cols], in0=n[:, rows, vector_cols], in1=h[:, rows, vector_cols],
                        op=ALU.subtract,
                    )
                if another_unit:
                    make_dn(rows)

            dn_grouped = grouped_tile("dn_grouped")
            dz_grouped = grouped_tile("dz_grouped")

            def make_dz_from_sbuf(c):
                rows = rows_of_pass[c]
                if vector_cols.stop > 0:
                    nc.vector.tensor_tensor(
                        out=grouped_by_runs(dz_grouped[:, c, vector_cols, :]), in0=by_runs(mz[:, rows, vector_cols]),
                        in1=by_runs(d_rows[:, rows, vector_cols]), op=ALU.mult,
                    )

            for c, rows in enumerate(rows_of_pass):
                if not (another_unit and c < last_pass):
                    make_dn(rows)
                nc.scalar.copy(out=grouped_by_runs(dn_grouped[:, c, :, :]), in_=by_runs(dn[:, rows, :]))
                if another_unit and c < last_pass:
                    make_dz_from_sbuf(c)
            if not another_unit:
                for c in passes[:-1]:
                    make_dz_from_sbuf(c)
                d_late = sbuf.tile([P, PACK, GPSIMD_COLUMNS], F32, name="d_late", tag="m")
                nc.gpsimd.tensor_tensor(
                    out=d_late[:], in0=n[:, rows_of_pass[0], extra_cols], in1=h[:, rows_of_pass[0], extra_cols],
                    op=ALU.subtract,
                )
            hrr = r
            for rows in rows_of_pass:
                nc.scalar.activation(
                    out=flat(hrr[:, rows, :]), in_=flat(r[:, rows, :]), func=ACT.Square, bias=-0.5
                )
            if u == 0:
                for v in units:
                    for c in passes:
                        nc.scalar.copy(out=grouped_by_runs(x_grouped[v][:, c, :, :]), in_=by_runs(x[:, c, :, v, :]))

            for d_bank, cols in zip(extra_banks, bank_cols):
                nc.vector.tensor_tensor(
                    out=grouped_by_runs(dz_grouped[:, 0, cols, :]), in0=by_runs(mz[:, rows_of_pass[0], cols]),
                    in1=by_runs(d_bank[:]), op=ALU.mult,
                )
            d_more = sbuf.tile([P, PACK, P], F32, name="d_more") if vector_tiles else None
            for cols in vector_tiles:
                nc.vector.tensor_tensor(
                    out=d_more[:], in0=n[:, rows_of_pass[last_pass], cols], in1=h[:, rows_of_pass[last_pass], cols],
                    op=ALU.subtract,
                )
            for d_bank, cols in zip(d_banks, tensor_tiles):
                nc.vector.tensor_tensor(
                    out=grouped_by_runs(dz_grouped[:, last_pass, cols, :]),
                    in0=by_runs(mz[:, rows_of_pass[last_pass], cols]),
                    in1=by_runs(d_bank[:]),
                    op=ALU.mult,
                )
            for cols in vector_tiles:
                nc.vector.tensor_tensor(
                    out=grouped_by_runs(dz_grouped[:, last_pass, cols, :]),
                    in0=by_runs(mz[:, rows_of_pass[last_pass], cols]),
                    in1=by_runs(d_more[:]),
                    op=ALU.mult,
                )
            if another_unit:
                next_z_g_n_h = load_z_g_n_h(u + 1)
            else:
                nc.vector.tensor_tensor(
                    out=grouped_by_runs(dz_grouped[:, 0, extra_cols, :]),
                    in0=by_runs(mz[:, rows_of_pass[0], extra_cols]),
                    in1=by_runs(d_late[:]),
                    op=ALU.mult,
                )

            def make_hrr():
                for rows in rows_of_pass:
                    nc.vector.scalar_tensor_tensor(
                        out=flat(hrr[:, rows, :]), in0=flat(hrr[:, rows, :]), scalar=0.25,
                        in1=flat(hn_rows[:, rows, :]), op0=ALU.subtract, op1=ALU.mult,
                    )

            dr_grouped = grouped_tile("dr_grouped")

            def make_dr(piece):
                c, tiles = piece
                cols = slice(tiles[0] * P, (tiles[-1] + 1) * P)
                nc.vector.tensor_tensor(
                    out=grouped_by_runs(dr_grouped[:, c, cols, :]),
                    in0=by_runs(dn[:, rows_of_pass[c], cols]),
                    in1=by_runs(hrr[:, rows_of_pass[c], cols]),
                    op=ALU.mult,
                )

            if another_unit:
                quantise_gate(DN, dn_grouped)
                quantise_gate(DZ, dz_grouped)
                make_hrr()
                for c in passes:
                    make_dr((c, all_tiles))
                next_r_hn = load_r_hn(u + 1)
                quantise_x(u)
                quantise_gate(DR, dr_grouped)
                multiply_store(DN, 1.0)
                multiply_store(DZ, 1.0)
                dr_accs = multiply_all(DR)

                z, g, n, h = next_z_g_n_h
                r, hn_rows = next_r_hn
                dn = square_n(u + 1, n)
                store_all(DR, -1.0, dr_accs)
            else:
                quantise_gate(DN, dn_grouped)
                multiply_store(DN, 1.0)
                quantise_gate(DZ, dz_grouped)
                multiply_store(DZ, 1.0)
                make_hrr()

                dr_accs = open_banks()

                def finish_dr(piece):
                    c, tiles = piece
                    quantise(DR, c, dr_grouped, slice(tiles[0] * P, (tiles[-1] + 1) * P))
                    if c < last_pass:
                        for t in tiles[:AHEAD]:
                            multiply(DR, c, dr_accs[t], column_tiles[t])
                    else:
                        for t in tiles:
                            multiply(DR, c, dr_accs[t], column_tiles[t])
                            store(DR, -1.0, dr_accs[t], column_tiles[t])
                            if t + AHEAD < len(column_tiles):
                                multiply(DR, 0, dr_accs[t + AHEAD], column_tiles[t + AHEAD])

                whole_passes = [(c, all_tiles) for c in passes[:-1]]
                tiles_of_last_pass = [(last_pass, [t]) for t in all_tiles]
                one_behind(whole_passes + tiles_of_last_pass, make_dr, finish_dr)
